import numpy as np
import ml_dtypes


def mxq(x, axis, fmt="e4m3"):
    dtype, down = {"e4m3": (ml_dtypes.float8_e4m3fn, 7), "e5m2": (ml_dtypes.float8_e5m2, 14)}[fmt]
    v = np.moveaxis(np.asarray(x, np.float32).astype(ml_dtypes.bfloat16).astype(np.float64), axis, -1)
    blocks = v.reshape(v.shape[:-1] + (-1, 32))
    amax = np.abs(blocks).max(-1, keepdims=True)
    byte = np.maximum(np.where(amax > 0, np.frexp(amax)[1] - 1 + 127, 0) - down, 1)
    scale = np.exp2(byte - 127.0)
    codes = (blocks / scale).astype(np.float32).astype(dtype).astype(np.float64)
    return np.moveaxis((codes * scale).reshape(v.shape), -1, axis)


WIDE = False


def mx_kscale(k):
    if not WIDE:
        return np.ones(k)
    levels = np.array([10, -10, 5, -5, 0])
    if k % 512:
        return np.exp2(np.random.permutation(np.resize(levels, k // 32))).repeat(32)
    a = np.empty((k // 512, 16))
    for p in range(k // 512):
        a[p, :8] = np.random.permutation(np.resize(levels, 8))
        for g in range(8):
            far = levels[np.abs(levels - a[p, g]) >= 10]
            a[p, g + 8] = far[np.random.randint(len(far))]
    return np.exp2(a.ravel()).repeat(32)


BF16 = ml_dtypes.bfloat16


def bf(x):
    return np.asarray(x, np.float32).astype(BF16)


def f64(x):
    return np.asarray(x).astype(np.float64)


B, S, HID, NH, NG, HD, QB = 1, 1024, 1024, 16, 2, 128, 512
QSZ = NH * HD
KVSZ = NG * HD
QKV = QSZ + 2 * KVSZ
ROT = HD // 2
RP = ROT // 2


def rope(x, cache):
    b, nh, sq, hn = x.shape
    xr, x_pass = x[..., :ROT], x[..., ROT:]
    xs = xr.reshape(b, nh, sq, RP, 2)
    c = cache[:, :sq].reshape(-1, 1, sq, RP, 2)
    rot = np.stack([xs[..., 0] * c[..., 0] - xs[..., 1] * c[..., 1],
                    xs[..., 1] * c[..., 0] + xs[..., 0] * c[..., 1]], axis=-1)
    return np.concatenate([rot.reshape(b, nh, sq, ROT), x_pass], axis=-1)


def draw0():
    s = mx_kscale(HID)
    return {"hidden_states": bf(np.random.standard_normal((B, S, HID)) * s),
            "rope_cache": bf(np.random.standard_normal((1, S, RP, 2))),
            "w_qkv": bf(np.random.standard_normal((HID, QKV)) / np.sqrt(HID) / s[:, None]),
            "b_qkv": bf(np.random.standard_normal(QKV) * 0.5)}


def core(hidden_states, rope_cache, w_qkv, b_qkv):
    mixed = (mxq(f64(hidden_states), 2, "e4m3") @ mxq(f64(w_qkv), 0, "e4m3")) + f64(b_qkv)
    q = mixed[..., :QSZ].reshape(B, S, NH, HD).transpose(0, 2, 1, 3)
    k = mixed[..., QSZ:QSZ + KVSZ].reshape(B, S, NG, HD).transpose(0, 2, 1, 3)
    v = mixed[..., QSZ + KVSZ:].reshape(B, S, NG, HD).transpose(0, 2, 1, 3)
    c = f64(rope_cache)
    return rope(q, c), rope(k, c), v


def e4m3fn_bytes(y):
    return np.clip(np.asarray(y, np.float64), -448.0, 448.0).astype(np.float32).astype(ml_dtypes.float8_e4m3fn).view(np.uint8)


def e4m3fn_values(b):
    return np.asarray(b, np.uint8).view(ml_dtypes.float8_e4m3fn).astype(np.float64)


def setup_inputs():
    d = draw0()
    x0 = np.asarray(d['w_qkv']).astype(np.float64)
    s = (np.max(np.abs(x0), axis=(1,), keepdims=True) / 448.0).astype(np.float32)
    out = {}
    for k, v in d.items():
        if k == 'w_qkv':
            out['w_qkv_bytes'] = e4m3fn_bytes(x0 / s.astype(np.float64))
            out['w_qkv_scale'] = s
        else:
            out[k] = v
    return out


def reference(hidden_states, rope_cache, w_qkv_bytes, w_qkv_scale, b_qkv):
    return core(hidden_states, rope_cache, e4m3fn_values(w_qkv_bytes) * w_qkv_scale.astype(np.float64), b_qkv)

@@ -1,0 +1,328 @@
+from contextlib import ExitStack
+
+import concourse.mybir as mybir
+from concourse.masks import make_identity
+
+F32 = mybir.dt.float32
+BF16 = mybir.dt.bfloat16
+U32 = mybir.dt.uint32
+U8 = mybir.dt.uint8
+FP8 = mybir.dt.float8_e4m3fn
+FP8X4 = mybir.dt.float8_e4m3fn_x4
+ALU = mybir.AluOpType
+ACT = mybir.ActivationFunctionType
+
+P = 128
+FLOPS = 2 * 1024 * 1024 * 2560
+
+
+def tile_selfattention_pa_kernel(
+    tc, hidden_states, rope_cache, w_qkv_bytes, w_qkv_scale, b_qkv, out_0, out_1, out_2
+):
+    nc = tc.nc
+    with ExitStack() as ctx:
+        const = ctx.enter_context(tc.tile_pool(name="const", bufs=1))
+        stream = ctx.enter_context(tc.tile_pool(name="stream", bufs=2))
+        psum = ctx.enter_context(tc.psum_pool(name="psum", bufs=2))
+
+        wsc = const.tile([P, 8], F32, name="wsc")
+        nc.sync.dma_start(
+            out=wsc[:].rearrange("p (g t) -> p g t", g=2),
+            in_=w_qkv_scale.rearrange("(g p t) o -> p g (t o)", p=P, t=4),
+        )
+        cs = const.tile([P, 8, 64], BF16, name="cs")
+        nc.sync.dma_start(out=cs[:], in_=rope_cache.rearrange("o (p i) j e -> (o p) i (j e)", i=8))
+
+        w_view = w_qkv_bytes.rearrange("(g p t) n -> g p t n", p=P, t=4)
+        wb = []
+
+        def load_w(c):
+            t = const.tile([P, 8, 512], U8, name="wbytes%d" % c)
+            for g in range(2):
+                nc.sync.dma_start(out=t[:, 4 * g : 4 * g + 4, :], in_=w_view[g, :, :, 512 * c : 512 * (c + 1)])
+            wb.append(t)
+
+        x_view = hidden_states.rearrange("o (p i) k -> (o p) i k", i=8)
+        xs = []
+
+        def load_x(q):
+            t = const.tile([P, 4, 1024], BF16, name="xs%d" % q)
+            nc.sync.dma_start(out=t[:], in_=x_view[:, 4 * q : 4 * q + 4, :])
+            xs.append(t)
+
+        load_w(0)
+        load_x(0)
+        load_x(1)
+        load_w(1)
+        b_rot = const.tile([P, 9], BF16, name="b_rot")
+        b_cols = b_qkv.rearrange("(r x) -> x r", x=256)
+        with nc.allow_non_contiguous_dma(reason="one bias element to a partition"):
+            for hh in range(2):
+                nc.sync.dma_start(out=b_rot[64 * hh : 64 * hh + 64, :], in_=b_cols[128 * hh : 128 * hh + 64, 0:9])
+        load_w(2)
+        bias_bc = const.tile([P, 2560], BF16, name="bias_bc")
+        nc.sync.dma_start(out=bias_bc[:], in_=b_qkv.partition_broadcast(P))
+        load_w(3)
+        load_w(4)
+
+        warm = const.tile([P, 2], F32, name="warm")
+        nc.vector.memset(warm[:, 0:1], 0.0)
+        nc.scalar.activation(out=warm[:, 1:2], in_=warm[:, 0:1], func=ACT.Copy)
+
+        ident_f = const.tile([P, P], F32, name="ident_f")
+        make_identity(nc, ident_f[:])
+        ident_b = const.tile([P, P], BF16, name="ident_b")
+        make_identity(nc, ident_b[:])
+        perm_f = const.tile([P, P], F32, name="perm_f")
+        id_pairs = ident_f[:].rearrange("p (m e) -> p m e", e=2)
+        pm_pairs = perm_f[:].rearrange("p (m e) -> p m e", e=2)
+        nc.gpsimd.tensor_copy(out=pm_pairs[:, :, 0], in_=id_pairs[:, :, 1])
+        nc.gpsimd.tensor_copy(out=pm_pairs[:, :, 1], in_=id_pairs[:, :, 0])
+
+        def widen_ops(c, planes, vector_share):
+            ops = []
+            for gt in range(8):
+                def op(gt=gt):
+                    src = wb[c][:, gt, :].bitcast(FP8)
+                    if gt in vector_share:
+                        nc.vector.tensor_scalar(
+                            out=planes[:, gt, :], in0=src, scalar1=wsc[:, gt : gt + 1], scalar2=None, op0=ALU.mult
+                        )
+                    else:
+                        nc.scalar.activation(out=planes[:, gt, :], in_=src, func=ACT.Copy, scale=wsc[:, gt : gt + 1])
+                ops.append(op)
+            return ops
+
+        def interleave_ops(c, planes, grouped, on_vector):
+            ops = []
+            for g in range(2):
+                src = planes[:, 4 * g : 4 * g + 4, :]
+                dst = grouped[:, g, :]
+                pairs = []
+                if c < 4:
+                    sv = src.rearrange("p t (h f c) -> p f h c t", f=2, c=64)
+                    for f in range(2):
+                        pairs.append((dst[:, 1024 * f : 1024 * (f + 1)].rearrange("p (h c t) -> p h c t", h=4, t=4), sv[:, f]))
+                else:
+                    sv = src[:, :, 0:256].rearrange("p t (h f c) -> p f h c t", f=2, c=64)
+                    for f in range(2):
+                        pairs.append((dst[:, 512 * f : 512 * (f + 1)].rearrange("p (h c t) -> p h c t", h=2, t=4), sv[:, f]))
+                    pairs.append((dst[:, 1024:2048].rearrange("p (n t) -> p n t", t=4), src[:, :, 256:512].rearrange("p t n -> p n t")))
+                for d, s in pairs:
+                    def op(d=d, s=s):
+                        if on_vector:
+                            nc.vector.tensor_copy(out=d, in_=s)
+                        else:
+                            nc.gpsimd.tensor_scalar(out=d, in0=s, scalar1=1.0, scalar2=0.0, op0=ALU.mult, op1=ALU.add)
+                    ops.append(op)
+            return ops
+
+        def quantize_w(grouped, codes, scales, g):
+            nc.vector.quantize_mx(out=codes[:, g, :].bitcast(FP8X4), scales=scales[:, g, :], in_=grouped[:, g, :])
+
+        def new_planes():
+            return stream.tile([P, 8, 512], BF16, name="planes", tag="planes")
+
+        def new_grouped():
+            return stream.tile([P, 2, 2048], BF16, name="grouped", tag="grouped", align_bytes=64)
+
+        def new_codes():
+            wc = stream.tile([P, 2, 512], U32, name="wcodes", tag="wcodes", align_bytes=64)
+            wsl = stream.tile([P, 2, 512], U8, name="wscales", tag="wscales", align_bytes=64)
+            return wc, wsl
+
+        planes_of = {}
+        grouped_of = {}
+        codes_of = {}
+
+        planes_of[0] = new_planes()
+        for op in widen_ops(0, planes_of[0], (4, 5, 6, 7)):
+            op()
+
+        ctm = const.tile([P, 2, 8, P], BF16, name="ctm")
+        cs4 = cs[:].rearrange("p i (j e) -> p i j e", e=2)
+        for hh in range(2):
+            d0 = ctm[:, 0, :, 64 * hh : 64 * hh + 64].rearrange("p i (j e) -> p i j e", e=2)
+            nc.gpsimd.tensor_scalar(
+                out=d0, in0=cs4[:, :, :, 0:1].to_broadcast([P, 8, 32, 2]), scalar1=1.0, scalar2=0.0, op0=ALU.mult, op1=ALU.add
+            )
+            d1 = ctm[:, 1, :, 64 * hh : 64 * hh + 64].rearrange("p i (j e) -> p i j e", e=2)
+            for e in range(2):
+                nc.gpsimd.tensor_scalar(
+                    out=d1[:, :, :, e], in0=cs4[:, :, :, 1], scalar1=(1.0 if e == 0 else -1.0), scalar2=0.0,
+                    op0=ALU.mult, op1=ALU.add,
+                )
+
+        grouped_of[0] = new_grouped()
+        codes_of[0] = new_codes()
+        il0 = interleave_ops(0, planes_of[0], grouped_of[0], True)
+        il0[2]()
+        il0[3]()
+        il0[0]()
+        quantize_w(grouped_of[0], codes_of[0][0], codes_of[0][1], 1)
+        il0[1]()
+
+        h_codes = const.tile([P, 2, 1024], U32, name="h_codes", align_bytes=64)
+        h_scales = const.tile([P, 2, 1024], U8, name="h_scales", align_bytes=64)
+        ct = const.tile([P, 2, 2, 512], BF16, name="ct")
+
+        def hidden_half(q):
+            hg = const.tile([P, 2, 4, P, 2], F32, name="hg%d" % q, align_bytes=64)
+            for i4 in range(4):
+                words = xs[q][:, i4, :].bitcast(F32)
+                xt = psum.tile([P, 2, 2, P], F32, name="xt", tag="tr")
+                for g in range(2):
+                    for u in range(2):
+                        nc.tensor.transpose(xt[:, g, u, :], words[:, 256 * g + u : 256 * (g + 1) : 2], ident_f[:])
+                nc.scalar.copy(out=hg[:, :, i4, :, :], in_=xt[:].rearrange("p g u r -> p g r u"))
+            return hg
+
+        def quantize_h(hg, q):
+            for g in range(2):
+                nc.vector.quantize_mx(
+                    out=h_codes[:, g, 512 * q : 512 * (q + 1)].bitcast(FP8X4),
+                    scales=h_scales[:, g, 512 * q : 512 * (q + 1)],
+                    in_=hg[:, g].rearrange("p i r u -> p (i r u)").bitcast(BF16),
+                )
+
+        def table_half(q):
+            ctp = psum.tile([P, 2, 4, P], BF16, name="ctp", tag="tr")
+            for tb in range(2):
+                for i4 in range(4):
+                    nc.tensor.transpose(ctp[:, tb, i4, :], ctm[:, tb, 4 * q + i4, :], ident_b[:])
+            nc.scalar.copy(out=ct[:, q], in_=ctp[:].rearrange("p b i r -> p b (i r)"))
+
+        hg0 = hidden_half(0)
+        quantize_w(grouped_of[0], codes_of[0][0], codes_of[0][1], 0)
+        quantize_h(hg0, 0)
+        table_half(0)
+        hg1 = hidden_half(1)
+        table_half(1)
+        quantize_h(hg1, 1)
+
+        planes_of[1] = new_planes()
+        for op in widen_ops(1, planes_of[1], ()):
+            op()
+
+        q_view = out_0.rearrange("o h (p i) c -> p (o h) (i c)", i=8)
+        k_view = out_1.rearrange("o h (p i) c -> p (o h) (i c)", i=8)
+        v_view = out_2.rearrange("o h (p i) c -> p (o h) (i c)", i=8)
+
+        def mx_group(out, lhsT, lhsT_s, rhs, rhs_s):
+            for g in range(2):
+                nc.tensor.matmul_mx(
+                    out=out,
+                    lhsT=lhsT(g).bitcast(FP8X4), lhsT_scale=lhsT_s(g),
+                    rhs=rhs(g).bitcast(FP8X4), rhs_scale=rhs_s(g),
+                    start=(g == 0), stop=(g == 1),
+                )
+
+        for c in range(5):
+            wc, wsl = codes_of[c]
+            res = stream.tile([P, 4, 8, P], F32, name="res", tag="res", bufs=3)
+
+            if c + 1 < 5:
+                grouped_of[c + 1] = new_grouped()
+                codes_of[c + 1] = new_codes()
+                il = interleave_ops(c + 1, planes_of[c + 1], grouped_of[c + 1], False)
+            else:
+                il = []
+            if c + 2 < 5:
+                planes_of[c + 2] = new_planes()
+                wd = widen_ops(c + 2, planes_of[c + 2], ())
+            else:
+                wd = []
+            for op in il:
+                op()
+
+            def rot_mx(rl, q):
+                bank = psum.tile([P, 512], F32, name="rotb", tag="rot")
+                mx_group(
+                    bank[:],
+                    lambda g: wc[:, g, P * rl : P * (rl + 1)], lambda g: wsl[:, g, P * rl : P * (rl + 1)],
+                    lambda g: h_codes[:, g, 512 * q : 512 * (q + 1)], lambda g: h_scales[:, g, 512 * q : 512 * (q + 1)],
+                )
+                return bank
+
+            def rot_mul(bank, rl, q):
+                r = 2 * c + rl
+                ab = stream.tile([P, 2, 512], F32, name="ab", tag="ab", bufs=3)
+                nc.vector.scalar_tensor_tensor(
+                    out=ab[:], in0=bank[:].unsqueeze(1).to_broadcast([P, 2, 512]), scalar=b_rot[:, r : r + 1],
+                    in1=ct[:, q], op0=ALU.add, op1=ALU.mult,
+                )
+                return ab
+
+            def rot_back(ab, rl, q):
+                yb = psum.tile([P, 4, P], F32, name="yb", tag="y")
+                for i4 in range(4):
+                    nc.tensor.matmul(out=yb[:, i4, :], lhsT=ab[:, 0, P * i4 : P * (i4 + 1)], rhs=ident_f[:],
+                                     is_transpose=True, start=True, stop=False)
+                    nc.tensor.matmul(out=yb[:, i4, :], lhsT=ab[:, 1, P * i4 : P * (i4 + 1)], rhs=perm_f[:],
+                                     is_transpose=True, start=False, stop=True)
+                nc.scalar.copy(
+                    out=res[:, 2 * rl : 2 * rl + 2, 4 * q : 4 * q + 4, 0:64].rearrange("p h i c -> p i h c"),
+                    in_=yb[:].rearrange("p i (h c) -> p i h c", c=64),
+                )
+
+            def pass_step(col0, width, first_i, out_ap, bias_ap):
+                n_i = 512 // width
+                bank = psum.tile([P, n_i, width], F32, name="passb", tag="pass")
+                for ii in range(n_i):
+                    i = first_i + ii
+                    mx_group(
+                        bank[:, ii, :],
+                        lambda g: h_codes[:, g, P * i : P * (i + 1)], lambda g: h_scales[:, g, P * i : P * (i + 1)],
+                        lambda g: wc[:, g, col0 : col0 + width], lambda g: wsl[:, g, col0 : col0 + width],
+                    )
+                hc = bias_ap.shape[2]
+                nc.vector.tensor_tensor(
+                    out=out_ap, in0=bank[:].rearrange("p i (h c) -> p i h c", c=hc),
+                    in1=bias_ap.unsqueeze(1).to_broadcast([P, n_i, bias_ap.shape[1], hc]), op=ALU.add,
+                )
+
+            rot_list = [(rl, q) for rl in range(2 if c < 4 else 1) for q in range(2)]
+            pass_list = []
+            halves = bias_bc[:, 512 * c : 512 * (c + 1)]
+            if c < 4:
+                b_ap = halves.rearrange("p (h f c) -> p f h c", f=2, c=64)[:, 1]
+                for ip in range(4):
+                    pass_list.append((256, 256, 2 * ip, res[:, :, 2 * ip : 2 * ip + 2, 64:128].rearrange("p h i c -> p i h c"), b_ap))
+            else:
+                b_v = halves[:, 256:512].rearrange("p (h c) -> p h c", c=128)
+                for ip in range(4):
+                    pass_list.append((256, 256, 2 * ip, res[:, 2:4, 2 * ip : 2 * ip + 2, :].rearrange("p h i c -> p i h c"), b_v))
+                b_k = halves[:, 0:256].rearrange("p (h f c) -> p f h c", f=2, c=64)[:, 1]
+                for q in range(2):
+                    pass_list.append((128, 128, 4 * q, res[:, 0:2, 4 * q : 4 * q + 4, 64:128].rearrange("p h i c -> p i h c"), b_k))
+
+            pending = None
+            n_steps = max(len(rot_list), len(pass_list))
+            for s in range(n_steps):
+                bank = None
+                if s < len(rot_list):
+                    bank = rot_mx(*rot_list[s])
+                if s < len(pass_list):
+                    pass_step(*pass_list[s])
+                if pending is not None:
+                    rot_back(*pending)
+                    pending = None
+                if bank is not None:
+                    ab = rot_mul(bank, *rot_list[s])
+                    pending = (ab,) + rot_list[s]
+                for op in wd[2 * s : 2 * s + 2]:
+                    op()
+                if c + 1 < 5 and s >= 2 and s < 4:
+                    quantize_w(grouped_of[c + 1], codes_of[c + 1][0], codes_of[c + 1][1], s - 2)
+            if pending is not None:
+                rot_back(*pending)
+            for op in wd[2 * n_steps :]:
+                op()
+
+            flat = res[:].rearrange("p h i c -> p h (i c)")
+            if c < 4:
+                for rl in range(2):
+                    nc.sync.dma_start(out=q_view[:, 4 * c + 2 * rl : 4 * c + 2 * rl + 2, :], in_=flat[:, 2 * rl : 2 * rl + 2, :])
+            else:
+                nc.sync.dma_start(out=v_view[:, :, :], in_=flat[:, 2:4, :])
+                nc.sync.dma_start(out=k_view[:, :, :], in_=flat[:, 0:2, :])

@@ -289,12 +289,12 @@ def tile_selfattention_pa_kernel(
                 for ip in range(4):
                     pass_list.append((256, 256, 2 * ip, res[:, :, 2 * ip : 2 * ip + 2, 64:128].rearrange("p h i c -> p i h c"), b_ap))
             else:
-                b_v = halves[:, 256:512].rearrange("p (h c) -> p h c", c=128)
-                for ip in range(4):
-                    pass_list.append((256, 256, 2 * ip, res[:, 2:4, 2 * ip : 2 * ip + 2, :].rearrange("p h i c -> p i h c"), b_v))
                 b_k = halves[:, 0:256].rearrange("p (h f c) -> p f h c", f=2, c=64)[:, 1]
                 for q in range(2):
                     pass_list.append((128, 128, 4 * q, res[:, 0:2, 4 * q : 4 * q + 4, 64:128].rearrange("p h i c -> p i h c"), b_k))
+                b_v = halves[:, 256:512].rearrange("p (h c) -> p h c", c=128)
+                for ip in range(4):
+                    pass_list.append((256, 256, 2 * ip, res[:, 2:4, 2 * ip : 2 * ip + 2, :].rearrange("p h i c -> p i h c"), b_v))
 
             pending = None
             n_steps = max(len(rot_list), len(pass_list))
@@ -312,6 +312,13 @@ def tile_selfattention_pa_kernel(
                     pending = (ab,) + rot_list[s]
                 for op in wd[2 * s : 2 * s + 2]:
                     op()
+                if c == 4 and s == 3:
+                    nc.sync.dma_start(out=k_view[:, :, :], in_=res[:].rearrange("p h i c -> p h (i c)")[:, 0:2, :])
+                if c == 4 and s >= 2:
+                    nc.sync.dma_start(
+                        out=v_view[:, :, 256 * (s - 2) : 256 * (s - 1)],
+                        in_=res[:].rearrange("p h i c -> p h (i c)")[:, 2:4, 256 * (s - 2) : 256 * (s - 1)],
+                    )
                 if c + 1 < 5 and s >= 2 and s < 4:
                     quantize_w(grouped_of[c + 1], codes_of[c + 1][0], codes_of[c + 1][1], s - 2)
             if pending is not None:
@@ -323,6 +330,3 @@ def tile_selfattention_pa_kernel(
             if c < 4:
                 for rl in range(2):
                     nc.sync.dma_start(out=q_view[:, 4 * c + 2 * rl : 4 * c + 2 * rl + 2, :], in_=flat[:, 2 * rl : 2 * rl + 2, :])
-            else:
-                nc.sync.dma_start(out=v_view[:, :, :], in_=flat[:, 2:4, :])
-                nc.sync.dma_start(out=k_view[:, :, :], in_=flat[:, 0:2, :])

@@ -217,116 +217,163 @@ def tile_selfattention_pa_kernel(
                     start=(g == 0), stop=(g == 1),
                 )
 
-        for c in range(5):
+        def rot_mx(c, rl, q):
             wc, wsl = codes_of[c]
-            res = stream.tile([P, 4, 8, P], F32, name="res", tag="res", bufs=3)
+            bank = psum.tile([P, 512], F32, name="rotb", tag="rot")
+            mx_group(
+                bank[:],
+                lambda g: wc[:, g, P * rl : P * (rl + 1)], lambda g: wsl[:, g, P * rl : P * (rl + 1)],
+                lambda g: h_codes[:, g, 512 * q : 512 * (q + 1)], lambda g: h_scales[:, g, 512 * q : 512 * (q + 1)],
+            )
+            return bank
 
-            if c + 1 < 5:
-                grouped_of[c + 1] = new_grouped()
-                codes_of[c + 1] = new_codes()
-                il = interleave_ops(c + 1, planes_of[c + 1], grouped_of[c + 1], False)
-            else:
-                il = []
-            if c + 2 < 5:
-                planes_of[c + 2] = new_planes()
-                wd = widen_ops(c + 2, planes_of[c + 2], ())
-            else:
-                wd = []
-            for op in il:
-                op()
+        def rot_mul(bank, c, rl, q):
+            r = 2 * c + rl
+            ab = stream.tile([P, 2, 512], F32, name="ab", tag="ab", bufs=4)
+            nc.vector.scalar_tensor_tensor(
+                out=ab[:], in0=bank[:].unsqueeze(1).to_broadcast([P, 2, 512]), scalar=b_rot[:, r : r + 1],
+                in1=ct[:, q], op0=ALU.add, op1=ALU.mult,
+            )
+            return ab
 
-            def rot_mx(rl, q):
-                bank = psum.tile([P, 512], F32, name="rotb", tag="rot")
+        def rot_back(ab):
+            yb = psum.tile([P, 4, P], F32, name="yb", tag="y")
+            for i4 in range(4):
+                nc.tensor.matmul(out=yb[:, i4, :], lhsT=ab[:, 0, P * i4 : P * (i4 + 1)], rhs=ident_f[:],
+                                 is_transpose=True, start=True, stop=False)
+                nc.tensor.matmul(out=yb[:, i4, :], lhsT=ab[:, 1, P * i4 : P * (i4 + 1)], rhs=perm_f[:],
+                                 is_transpose=True, start=False, stop=True)
+            return yb
+
+        def rot_evac(yb, out_ap):
+            nc.scalar.copy(out=out_ap.rearrange("p h i c -> p i h c"), in_=yb[:].rearrange("p i (h c) -> p i h c", c=64))
+
+        def pass_mx(c, col0, width, first_i):
+            wc, wsl = codes_of[c]
+            n_i = 512 // width
+            bank = psum.tile([P, n_i, width], F32, name="passb", tag="pass")
+            for ii in range(n_i):
+                i = first_i + ii
                 mx_group(
-                    bank[:],
-                    lambda g: wc[:, g, P * rl : P * (rl + 1)], lambda g: wsl[:, g, P * rl : P * (rl + 1)],
-                    lambda g: h_codes[:, g, 512 * q : 512 * (q + 1)], lambda g: h_scales[:, g, 512 * q : 512 * (q + 1)],
+                    bank[:, ii, :],
+                    lambda g: h_codes[:, g, P * i : P * (i + 1)], lambda g: h_scales[:, g, P * i : P * (i + 1)],
+                    lambda g: wc[:, g, col0 : col0 + width], lambda g: wsl[:, g, col0 : col0 + width],
                 )
-                return bank
+            return bank
 
-            def rot_mul(bank, rl, q):
-                r = 2 * c + rl
-                ab = stream.tile([P, 2, 512], F32, name="ab", tag="ab", bufs=3)
-                nc.vector.scalar_tensor_tensor(
-                    out=ab[:], in0=bank[:].unsqueeze(1).to_broadcast([P, 2, 512]), scalar=b_rot[:, r : r + 1],
-                    in1=ct[:, q], op0=ALU.add, op1=ALU.mult,
-                )
-                return ab
+        def pass_add(bank, out_ap, bias_ap):
+            hc = bias_ap.shape[2]
+            n_i = out_ap.shape[2]
+            nc.vector.tensor_tensor(
+                out=out_ap.rearrange("p h i c -> p i h c"), in0=bank[:].rearrange("p i (h c) -> p i h c", c=hc),
+                in1=bias_ap.unsqueeze(1).to_broadcast([P, n_i, bias_ap.shape[1], hc]), op=ALU.add,
+            )
 
-            def rot_back(ab, rl, q):
-                yb = psum.tile([P, 4, P], F32, name="yb", tag="y")
-                for i4 in range(4):
-                    nc.tensor.matmul(out=yb[:, i4, :], lhsT=ab[:, 0, P * i4 : P * (i4 + 1)], rhs=ident_f[:],
-                                     is_transpose=True, start=True, stop=False)
-                    nc.tensor.matmul(out=yb[:, i4, :], lhsT=ab[:, 1, P * i4 : P * (i4 + 1)], rhs=perm_f[:],
-                                     is_transpose=True, start=False, stop=True)
-                nc.scalar.copy(
-                    out=res[:, 2 * rl : 2 * rl + 2, 4 * q : 4 * q + 4, 0:64].rearrange("p h i c -> p i h c"),
-                    in_=yb[:].rearrange("p i (h c) -> p i h c", c=64),
-                )
+        def new_res(shape):
+            return stream.tile(shape, F32, name="res", tag="res", bufs=4)
 
-            def pass_step(col0, width, first_i, out_ap, bias_ap):
-                n_i = 512 // width
-                bank = psum.tile([P, n_i, width], F32, name="passb", tag="pass")
-                for ii in range(n_i):
-                    i = first_i + ii
-                    mx_group(
-                        bank[:, ii, :],
-                        lambda g: h_codes[:, g, P * i : P * (i + 1)], lambda g: h_scales[:, g, P * i : P * (i + 1)],
-                        lambda g: wc[:, g, col0 : col0 + width], lambda g: wsl[:, g, col0 : col0 + width],
-                    )
-                hc = bias_ap.shape[2]
-                nc.vector.tensor_tensor(
-                    out=out_ap, in0=bank[:].rearrange("p i (h c) -> p i h c", c=hc),
-                    in1=bias_ap.unsqueeze(1).to_broadcast([P, n_i, bias_ap.shape[1], hc]), op=ALU.add,
-                )
+        slots = []
+        for c in range(4):
+            b_ap = bias_bc[:, 512 * c : 512 * (c + 1)].rearrange("p (h f c) -> p f h c", f=2, c=64)[:, 1]
+            for q in range(2):
+                slots.append({"c": c, "q": q, "ropes": [(c, 0, q), (c, 1, q)], "kind": "q", "bias": b_ap})
+        slots.append({"c": 4, "kind": "k", "ropes": [(4, 0, 0), (4, 0, 1)]})
+        slots.append({"c": 4, "kind": "v", "ropes": []})
+        b_k = bias_bc[:, 2048:2304].rearrange("p (h f c) -> p f h c", f=2, c=64)[:, 1]
+        b_v = bias_bc[:, 2304:2560].rearrange("p (h c) -> p h c", c=128)
 
-            rot_list = [(rl, q) for rl in range(2 if c < 4 else 1) for q in range(2)]
-            pass_list = []
-            halves = bias_bc[:, 512 * c : 512 * (c + 1)]
-            if c < 4:
-                b_ap = halves.rearrange("p (h f c) -> p f h c", f=2, c=64)[:, 1]
-                for ip in range(4):
-                    pass_list.append((256, 256, 2 * ip, res[:, :, 2 * ip : 2 * ip + 2, 64:128].rearrange("p h i c -> p i h c"), b_ap))
-            else:
-                b_k = halves[:, 0:256].rearrange("p (h f c) -> p f h c", f=2, c=64)[:, 1]
-                for q in range(2):
-                    pass_list.append((128, 128, 4 * q, res[:, 0:2, 4 * q : 4 * q + 4, 64:128].rearrange("p h i c -> p i h c"), b_k))
-                b_v = halves[:, 256:512].rearrange("p (h c) -> p h c", c=128)
-                for ip in range(4):
-                    pass_list.append((256, 256, 2 * ip, res[:, 2:4, 2 * ip : 2 * ip + 2, :].rearrange("p h i c -> p i h c"), b_v))
+        il_of = {}
 
-            pending = None
-            n_steps = max(len(rot_list), len(pass_list))
-            for s in range(n_steps):
-                bank = None
-                if s < len(rot_list):
-                    bank = rot_mx(*rot_list[s])
-                if s < len(pass_list):
-                    pass_step(*pass_list[s])
-                if pending is not None:
-                    rot_back(*pending)
-                    pending = None
-                if bank is not None:
-                    ab = rot_mul(bank, *rot_list[s])
-                    pending = (ab,) + rot_list[s]
-                for op in wd[2 * s : 2 * s + 2]:
-                    op()
-                if c == 4 and s == 3:
-                    nc.sync.dma_start(out=k_view[:, :, :], in_=res[:].rearrange("p h i c -> p h (i c)")[:, 0:2, :])
-                if c == 4 and s >= 2:
-                    nc.sync.dma_start(
-                        out=v_view[:, :, 256 * (s - 2) : 256 * (s - 1)],
-                        in_=res[:].rearrange("p h i c -> p h (i c)")[:, 2:4, 256 * (s - 2) : 256 * (s - 1)],
-                    )
-                if c + 1 < 5 and s >= 2 and s < 4:
-                    quantize_w(grouped_of[c + 1], codes_of[c + 1][0], codes_of[c + 1][1], s - 2)
-            if pending is not None:
-                rot_back(*pending)
-            for op in wd[2 * n_steps :]:
+        def prep_widen(c, g):
+            if g == 0:
+                planes_of[c] = new_planes()
+            for op in widen_ops(c, planes_of[c], ())[4 * g : 4 * g + 4]:
                 op()
 
-            flat = res[:].rearrange("p h i c -> p h (i c)")
-            if c < 4:
-                for rl in range(2):
-                    nc.sync.dma_start(out=q_view[:, 4 * c + 2 * rl : 4 * c + 2 * rl + 2, :], in_=flat[:, 2 * rl : 2 * rl + 2, :])
+        def prep_interleave(c, g):
+            if g == 0:
+                grouped_of[c] = new_grouped()
+                il_of[c] = interleave_ops(c, planes_of[c], grouped_of[c], False)
+            n = len(il_of[c]) // 2
+            for op in il_of[c][n * g : n * (g + 1)]:
+                op()
+
+        def prep_quantize(c, g):
+            if g == 0:
+                codes_of[c] = new_codes()
+            quantize_w(grouped_of[c], codes_of[c][0], codes_of[c][1], g)
+
+        prep_interleave(1, 0)
+        prep_interleave(1, 1)
+
+        ctx.enter_context(tc.manual_schedule())
+        prev = None
+        for k in range(len(slots)):
+            sl = slots[k]
+            c = sl["c"]
+            early_q = []
+            late_q = []
+            for cw in range(1, 5):
+                for g in range(2):
+                    if 2 * cw - 2 + g == k:
+                        if cw == 1:
+                            late_q.append((cw, g))
+                        else:
+                            early_q.append((cw, g))
+            for cw, g in early_q:
+                prep_quantize(cw, g)
+            for cw in range(2, 5):
+                for g in range(2):
+                    if 2 * cw - 4 + g == k:
+                        prep_widen(cw, g)
+                    if 2 * cw - 3 + g == k:
+                        prep_interleave(cw, g)
+            banks = [rot_mx(*u) for u in sl["ropes"]]
+            adds = []
+            if sl["kind"] == "q":
+                q = sl["q"]
+                res = new_res([P, 4, 4, P])
+                sl["res"] = res
+                for ipl in range(2):
+                    adds.append((pass_mx(c, 256, 256, 4 * q + 2 * ipl), res[:, :, 2 * ipl : 2 * ipl + 2, 64:128], sl["bias"]))
+            elif sl["kind"] == "k":
+                res = new_res([P, 2, 8, P])
+                sl["res"] = res
+                for q in range(2):
+                    adds.append((pass_mx(4, 128, 128, 4 * q), res[:, :, 4 * q : 4 * q + 4, 64:128], b_k))
+            else:
+                res = new_res([P, 2, 8, P])
+                sl["res"] = res
+                for ip in range(2):
+                    adds.append((pass_mx(4, 256, 256, 2 * ip), res[:, :, 2 * ip : 2 * ip + 2, :], b_v))
+            if prev is not None and prev["ropes"]:
+                ybs = [rot_back(ab) for ab in prev["abs"]]
+                pres = prev["res"]
+                for j in range(len(ybs)):
+                    if prev["kind"] == "q":
+                        rot_evac(ybs[j], pres[:, 2 * j : 2 * j + 2, :, 0:64])
+                    else:
+                        rot_evac(ybs[j], pres[:, :, 4 * j : 4 * j + 4, 0:64])
+                flat = pres[:].rearrange("p h i c -> p h (i c)")
+                if prev["kind"] == "q":
+                    pc = prev["c"]
+                    pq = prev["q"]
+                    nc.sync.dma_start(out=q_view[:, 4 * pc : 4 * pc + 4, 512 * pq : 512 * (pq + 1)], in_=flat)
+                else:
+                    nc.sync.dma_start(out=k_view[:, :, :], in_=flat)
+            if sl["kind"] == "v":
+                for ip in range(2, 4):
+                    adds.append((pass_mx(4, 256, 256, 2 * ip), res[:, :, 2 * ip : 2 * ip + 2, :], b_v))
+            sl["abs"] = [rot_mul(banks[j], *sl["ropes"][j]) for j in range(len(banks))]
+            n_add = 0
+            for bank, out_ap, bias_ap in adds:
+                pass_add(bank, out_ap, bias_ap)
+                if sl["kind"] == "v":
+                    nc.sync.dma_start(
+                        out=v_view[:, :, 256 * n_add : 256 * (n_add + 1)],
+                        in_=res[:].rearrange("p h i c -> p h (i c)")[:, :, 256 * n_add : 256 * (n_add + 1)],
+                    )
+                n_add += 1
+            for cw, g in late_q:
+                prep_quantize(cw, g)
+            prev = sl

@@ -93,11 +93,11 @@ def tile_selfattention_pa_kernel(
                 ops.append(op)
             return ops
 
-        def interleave_ops(c, planes, grouped, on_vector):
+        def interleave_ops(c, planes, grouped, on_vector, passes=(0, 1)):
             ops = []
-            for g in range(2):
+            for g in passes:
                 src = planes[:, 4 * g : 4 * g + 4, :]
-                dst = grouped[:, g, :]
+                dst = grouped[:, g if len(passes) == 2 else 0, :]
                 pairs = []
                 if c < 4:
                     sv = src.rearrange("p t (h f c) -> p f h c t", f=2, c=64)
@@ -124,7 +124,10 @@ def tile_selfattention_pa_kernel(
             return stream.tile([P, 8, 512], BF16, name="planes", tag="planes")
 
         def new_grouped():
-            return stream.tile([P, 2, 2048], BF16, name="grouped", tag="grouped", align_bytes=64)
+            return const.tile([P, 2, 2048], BF16, name="grouped0", align_bytes=64)
+
+        def new_grouped_half():
+            return stream.tile([P, 1, 2048], BF16, name="grouped", tag="grouped", align_bytes=64, bufs=1)
 
         def new_codes():
             wc = stream.tile([P, 2, 512], U32, name="wcodes", tag="wcodes", align_bytes=64)
@@ -291,43 +294,28 @@ def tile_selfattention_pa_kernel(
                 op()
 
         def prep_interleave(c, g):
-            if g == 0:
-                grouped_of[c] = new_grouped()
-                il_of[c] = interleave_ops(c, planes_of[c], grouped_of[c], False)
-            n = len(il_of[c]) // 2
-            for op in il_of[c][n * g : n * (g + 1)]:
+            il_of[(c, g)] = new_grouped_half()
+            for op in interleave_ops(c, planes_of[c], il_of[(c, g)], False, (g,)):
                 op()
 
         def prep_quantize(c, g):
             if g == 0:
                 codes_of[c] = new_codes()
-            quantize_w(grouped_of[c], codes_of[c][0], codes_of[c][1], g)
+            nc.vector.quantize_mx(
+                out=codes_of[c][0][:, g, :].bitcast(FP8X4), scales=codes_of[c][1][:, g, :], in_=il_of[(c, g)][:, 0, :]
+            )
 
         prep_interleave(1, 0)
-        prep_interleave(1, 1)
 
         ctx.enter_context(tc.manual_schedule())
         prev = None
         for k in range(len(slots)):
             sl = slots[k]
             c = sl["c"]
-            early_q = []
-            late_q = []
-            for cw in range(1, 5):
-                for g in range(2):
-                    if 2 * cw - 2 + g == k:
-                        if cw == 1:
-                            late_q.append((cw, g))
-                        else:
-                            early_q.append((cw, g))
-            for cw, g in early_q:
-                prep_quantize(cw, g)
             for cw in range(2, 5):
                 for g in range(2):
                     if 2 * cw - 4 + g == k:
                         prep_widen(cw, g)
-                    if 2 * cw - 3 + g == k:
-                        prep_interleave(cw, g)
             banks = [rot_mx(*u) for u in sl["ropes"]]
             adds = []
             if sl["kind"] == "q":
@@ -365,6 +353,10 @@ def tile_selfattention_pa_kernel(
                 for ip in range(2, 4):
                     adds.append((pass_mx(4, 256, 256, 2 * ip), res[:, :, 2 * ip : 2 * ip + 2, :], b_v))
             sl["abs"] = [rot_mul(banks[j], *sl["ropes"][j]) for j in range(len(banks))]
+            if k < 8:
+                prep_quantize(1 + k // 2, k % 2)
+            if k < 7:
+                prep_interleave(1 + (k + 1) // 2, (k + 1) % 2)
             n_add = 0
             for bank, out_ap, bias_ap in adds:
                 pass_add(bank, out_ap, bias_ap)
@@ -374,6 +366,4 @@ def tile_selfattention_pa_kernel(
                         in_=res[:].rearrange("p h i c -> p h (i c)")[:, :, 256 * n_add : 256 * (n_add + 1)],
                     )
                 n_add += 1
-            for cw, g in late_q:
-                prep_quantize(cw, g)
             prev = sl

@@ -139,8 +139,9 @@ def tile_selfattention_pa_kernel(
         codes_of = {}
 
         planes_of[0] = new_planes()
-        for op in widen_ops(0, planes_of[0], (4, 5, 6, 7)):
-            op()
+        w0_ops = widen_ops(0, planes_of[0], (6, 7))
+        for gt in (4, 5, 6, 7, 0, 1, 2, 3):
+            w0_ops[gt]()
 
         ctm = const.tile([P, 2, 8, P], BF16, name="ctm")
         cs4 = cs[:].rearrange("p i (j e) -> p i j e", e=2)
@@ -199,12 +200,14 @@ def tile_selfattention_pa_kernel(
         quantize_w(grouped_of[0], codes_of[0][0], codes_of[0][1], 0)
         quantize_h(hg0, 0)
         table_half(0)
+        planes_of[1] = new_planes()
+        w1_ops = widen_ops(1, planes_of[1], ())
+        for op in w1_ops[0:4]:
+            op()
         hg1 = hidden_half(1)
         table_half(1)
         quantize_h(hg1, 1)
-
-        planes_of[1] = new_planes()
-        for op in widen_ops(1, planes_of[1], ()):
+        for op in w1_ops[4:8]:
             op()
 
         q_view = out_0.rearrange("o h (p i) c -> p (o h) (i c)", i=8)
@@ -337,18 +340,17 @@ def tile_selfattention_pa_kernel(
             if prev is not None and prev["ropes"]:
                 ybs = [rot_back(ab) for ab in prev["abs"]]
                 pres = prev["res"]
+                flat = pres[:].rearrange("p h i c -> p h (i c)")
                 for j in range(len(ybs)):
                     if prev["kind"] == "q":
                         rot_evac(ybs[j], pres[:, 2 * j : 2 * j + 2, :, 0:64])
                     else:
                         rot_evac(ybs[j], pres[:, :, 4 * j : 4 * j + 4, 0:64])
-                flat = pres[:].rearrange("p h i c -> p h (i c)")
+                        nc.sync.dma_start(out=k_view[:, :, 512 * j : 512 * (j + 1)], in_=flat[:, :, 512 * j : 512 * (j + 1)])
                 if prev["kind"] == "q":
                     pc = prev["c"]
                     pq = prev["q"]
                     nc.sync.dma_start(out=q_view[:, 4 * pc : 4 * pc + 4, 512 * pq : 512 * (pq + 1)], in_=flat)
-                else:
-                    nc.sync.dma_start(out=k_view[:, :, :], in_=flat)
             if sl["kind"] == "v":
                 for ip in range(2, 4):
                     adds.append((pass_mx(4, 256, 256, 2 * ip), res[:, :, 2 * ip : 2 * ip + 2, :], b_v))

@@ -6,6 +6,7 @@ from concourse.masks import make_identity
 F32 = mybir.dt.float32
 BF16 = mybir.dt.bfloat16
 U32 = mybir.dt.uint32
+I32 = mybir.dt.int32
 U8 = mybir.dt.uint8
 FP8 = mybir.dt.float8_e4m3fn
 FP8X4 = mybir.dt.float8_e4m3fn_x4
@@ -32,6 +33,8 @@ def tile_selfattention_pa_kernel(
         )
         cs = const.tile([P, 8, 64], BF16, name="cs")
         nc.sync.dma_start(out=cs[:], in_=rope_cache.rearrange("o (p i) j e -> (o p) i (j e)", i=8))
+        bsel = const.tile([P, P], BF16, name="bsel")
+        nc.vector.memset(bsel[:].bitcast(I32), 0)
 
         w_view = w_qkv_bytes.rearrange("(g p t) n -> g p t n", p=P, t=4)
         wb = []
@@ -52,16 +55,15 @@ def tile_selfattention_pa_kernel(
 
         load_w(0)
         load_x(0)
+        nc.sync.dma_start(
+            out=bsel[0:9, :].rearrange("r (hh c) -> r hh c", hh=2),
+            in_=b_qkv[0:2304].rearrange("(r hh f c) -> r hh f c", hh=2, f=2, c=64)[:, :, 0, :],
+        )
         load_x(1)
         load_w(1)
-        b_rot = const.tile([P, 9], BF16, name="b_rot")
-        b_cols = b_qkv.rearrange("(r x) -> x r", x=256)
-        with nc.allow_non_contiguous_dma(reason="one bias element to a partition"):
-            for hh in range(2):
-                nc.sync.dma_start(out=b_rot[64 * hh : 64 * hh + 64, :], in_=b_cols[128 * hh : 128 * hh + 64, 0:9])
-        load_w(2)
         bias_bc = const.tile([P, 2560], BF16, name="bias_bc")
         nc.sync.dma_start(out=bias_bc[:], in_=b_qkv.partition_broadcast(P))
+        load_w(2)
         load_w(3)
         load_w(4)
 
@@ -78,6 +80,11 @@ def tile_selfattention_pa_kernel(
         pm_pairs = perm_f[:].rearrange("p (m e) -> p m e", e=2)
         nc.gpsimd.tensor_copy(out=pm_pairs[:, :, 0], in_=id_pairs[:, :, 1])
         nc.gpsimd.tensor_copy(out=pm_pairs[:, :, 1], in_=id_pairs[:, :, 0])
+
+        b_rot = const.tile([P, 9], BF16, name="b_rot")
+        btp = psum.tile([P, P], BF16, name="btp", tag="y")
+        nc.tensor.transpose(btp[:], bsel[:], ident_b[:])
+        nc.vector.tensor_copy(out=b_rot[:], in_=btp[:, 0:9])
 
         def widen_ops(c, planes, vector_share):
             ops = []

@@ -25,16 +25,21 @@ def tile_selfattention_pa_kernel(
         const = ctx.enter_context(tc.tile_pool(name="const", bufs=1))
         stream = ctx.enter_context(tc.tile_pool(name="stream", bufs=2))
         psum = ctx.enter_context(tc.psum_pool(name="psum", bufs=2))
+        ctx.enter_context(tc.manual_schedule())
+
+        zero = const.tile([P, 512], BF16, name="zero")
+        nc.vector.memset(zero[:].bitcast(I32), 0)
+        bsel = const.tile([P, P], BF16, name="bsel")
+        nc.vector.memset(bsel[:].bitcast(I32), 0)
+        warm = const.tile([P, 2], F32, name="warm")
+        nc.vector.memset(warm[:, 0:1], 0.0)
+        nc.scalar.activation(out=warm[:, 1:2], in_=warm[:, 0:1], func=ACT.Copy)
 
         wsc = const.tile([P, 8], F32, name="wsc")
         nc.sync.dma_start(
             out=wsc[:].rearrange("p (g t) -> p g t", g=2),
             in_=w_qkv_scale.rearrange("(g p t) o -> p g (t o)", p=P, t=4),
         )
-        cs = const.tile([P, 8, 64], BF16, name="cs")
-        nc.sync.dma_start(out=cs[:], in_=rope_cache.rearrange("o (p i) j e -> (o p) i (j e)", i=8))
-        bsel = const.tile([P, P], BF16, name="bsel")
-        nc.vector.memset(bsel[:].bitcast(I32), 0)
 
         w_view = w_qkv_bytes.rearrange("(g p t) n -> g p t n", p=P, t=4)
         wb = []
@@ -48,18 +53,22 @@ def tile_selfattention_pa_kernel(
         x_view = hidden_states.rearrange("o (p i) k -> (o p) i k", i=8)
         xs = []
 
-        def load_x(q):
-            t = const.tile([P, 4, 1024], BF16, name="xs%d" % q)
-            nc.sync.dma_start(out=t[:], in_=x_view[:, 4 * q : 4 * q + 4, :])
+        def load_x(h):
+            t = const.tile([P, 2, 1024], BF16, name="xs%d" % h)
+            nc.sync.dma_start(out=t[:], in_=x_view[:, 2 * h : 2 * h + 2, :])
             xs.append(t)
 
         load_w(0)
         load_x(0)
+        cs = const.tile([P, 8, 64], BF16, name="cs")
+        nc.sync.dma_start(out=cs[:], in_=rope_cache.rearrange("o (p i) j e -> (o p) i (j e)", i=8))
+        load_x(1)
         nc.sync.dma_start(
             out=bsel[0:9, :].rearrange("r (hh c) -> r hh c", hh=2),
             in_=b_qkv[0:2304].rearrange("(r hh f c) -> r hh f c", hh=2, f=2, c=64)[:, :, 0, :],
         )
-        load_x(1)
+        load_x(2)
+        load_x(3)
         load_w(1)
         bias_bc = const.tile([P, 2560], BF16, name="bias_bc")
         nc.sync.dma_start(out=bias_bc[:], in_=b_qkv.partition_broadcast(P))
@@ -67,155 +76,158 @@ def tile_selfattention_pa_kernel(
         load_w(3)
         load_w(4)
 
-        warm = const.tile([P, 2], F32, name="warm")
-        nc.vector.memset(warm[:, 0:1], 0.0)
-        nc.scalar.activation(out=warm[:, 1:2], in_=warm[:, 0:1], func=ACT.Copy)
-
         ident_f = const.tile([P, P], F32, name="ident_f")
         make_identity(nc, ident_f[:])
         ident_b = const.tile([P, P], BF16, name="ident_b")
         make_identity(nc, ident_b[:])
+
+        planes_of = {}
+        grouped_of = {}
+        codes_of = {}
+
+        def widen(c, gt, on_vector):
+            if c not in planes_of:
+                planes_of[c] = stream.tile([P, 8, 512], BF16, name="planes", tag="planes")
+            src = wb[c][:, gt, :].bitcast(FP8)
+            dst = planes_of[c][:, gt, :]
+            if on_vector:
+                nc.vector.tensor_scalar(out=dst, in0=src, scalar1=wsc[:, gt : gt + 1], scalar2=None, op0=ALU.mult)
+            else:
+                nc.scalar.activation(out=dst, in_=src, func=ACT.Copy, scale=wsc[:, gt : gt + 1])
+
+        def interleave(c, g, dst, on_vector):
+            grouped_of[(c, g)] = dst
+            src = planes_of[c][:, 4 * g : 4 * g + 4, :]
+            pairs = []
+            if c < 4:
+                sv = src.rearrange("p t (h f c) -> p f h c t", f=2, c=64)
+                for f in range(2):
+                    pairs.append((dst[:, 1024 * f : 1024 * (f + 1)].rearrange("p (h c t) -> p h c t", h=4, t=4), sv[:, f]))
+            else:
+                sv = src[:, :, 0:256].rearrange("p t (h f c) -> p f h c t", f=2, c=64)
+                for f in range(2):
+                    pairs.append((dst[:, 512 * f : 512 * (f + 1)].rearrange("p (h c t) -> p h c t", h=2, t=4), sv[:, f]))
+                pairs.append((dst[:, 1024:2048].rearrange("p (n t) -> p n t", t=4), src[:, :, 256:512].rearrange("p t n -> p n t")))
+            for d, s in pairs:
+                if on_vector:
+                    nc.vector.tensor_copy(out=d, in_=s)
+                else:
+                    nc.gpsimd.tensor_scalar(out=d, in0=s, scalar1=1.0, scalar2=0.0, op0=ALU.mult, op1=ALU.add)
+
+        def quantize_w(c, g):
+            if c not in codes_of:
+                wc = stream.tile([P, 2, 512], U32, name="wcodes", tag="wcodes", align_bytes=64, bufs=3)
+                wsl = stream.tile([P, 2, 512], U8, name="wscales", tag="wscales", align_bytes=64, bufs=3)
+                codes_of[c] = (wc, wsl)
+            nc.vector.quantize_mx(
+                out=codes_of[c][0][:, g, :].bitcast(FP8X4), scales=codes_of[c][1][:, g, :], in_=grouped_of[(c, g)]
+            )
+
+        own = const.tile([P, 2, 2048], BF16, name="own", align_bytes=64)
+
+        ctm = const.tile([P, 2, 8, P], BF16, name="ctm")
+        cs4 = cs[:].rearrange("p i (j e) -> p i j e", e=2)
+        def spread_table(q):
+            rows = slice(4 * q, 4 * q + 4)
+            for hh in range(2):
+                nc.vector.tensor_scalar(
+                    out=ctm[:, 0, rows, 64 * hh : 64 * hh + 64].rearrange("p i (j e) -> p i j e", e=2),
+                    in0=cs4[:, rows, :, 0:1].to_broadcast([P, 4, 32, 2]), scalar1=1.0, scalar2=0.0, op0=ALU.mult, op1=ALU.add,
+                )
+            dst = ctm[:, 1, rows, :].rearrange("p i (hh j e) -> p e i hh j", hh=2, e=2)
+            for e in range(2):
+                nc.vector.tensor_scalar(
+                    out=dst[:, e], in0=cs4[:, rows, :, 1].unsqueeze(2).to_broadcast([P, 4, 2, 32]),
+                    scalar1=(1.0 if e == 0 else -1.0), scalar2=0.0, op0=ALU.mult, op1=ALU.add,
+                )
+
         perm_f = const.tile([P, P], F32, name="perm_f")
         id_pairs = ident_f[:].rearrange("p (m e) -> p m e", e=2)
         pm_pairs = perm_f[:].rearrange("p (m e) -> p m e", e=2)
         nc.gpsimd.tensor_copy(out=pm_pairs[:, :, 0], in_=id_pairs[:, :, 1])
         nc.gpsimd.tensor_copy(out=pm_pairs[:, :, 1], in_=id_pairs[:, :, 0])
 
-        b_rot = const.tile([P, 9], BF16, name="b_rot")
-        btp = psum.tile([P, P], BF16, name="btp", tag="y")
-        nc.tensor.transpose(btp[:], bsel[:], ident_b[:])
-        nc.vector.tensor_copy(out=b_rot[:], in_=btp[:, 0:9])
-
-        def widen_ops(c, planes, vector_share):
-            ops = []
-            for gt in range(8):
-                def op(gt=gt):
-                    src = wb[c][:, gt, :].bitcast(FP8)
-                    if gt in vector_share:
-                        nc.vector.tensor_scalar(
-                            out=planes[:, gt, :], in0=src, scalar1=wsc[:, gt : gt + 1], scalar2=None, op0=ALU.mult
-                        )
-                    else:
-                        nc.scalar.activation(out=planes[:, gt, :], in_=src, func=ACT.Copy, scale=wsc[:, gt : gt + 1])
-                ops.append(op)
-            return ops
-
-        def interleave_ops(c, planes, grouped, on_vector, passes=(0, 1)):
-            ops = []
-            for g in passes:
-                src = planes[:, 4 * g : 4 * g + 4, :]
-                dst = grouped[:, g if len(passes) == 2 else 0, :]
-                pairs = []
-                if c < 4:
-                    sv = src.rearrange("p t (h f c) -> p f h c t", f=2, c=64)
-                    for f in range(2):
-                        pairs.append((dst[:, 1024 * f : 1024 * (f + 1)].rearrange("p (h c t) -> p h c t", h=4, t=4), sv[:, f]))
-                else:
-                    sv = src[:, :, 0:256].rearrange("p t (h f c) -> p f h c t", f=2, c=64)
-                    for f in range(2):
-                        pairs.append((dst[:, 512 * f : 512 * (f + 1)].rearrange("p (h c t) -> p h c t", h=2, t=4), sv[:, f]))
-                    pairs.append((dst[:, 1024:2048].rearrange("p (n t) -> p n t", t=4), src[:, :, 256:512].rearrange("p t n -> p n t")))
-                for d, s in pairs:
-                    def op(d=d, s=s):
-                        if on_vector:
-                            nc.vector.tensor_copy(out=d, in_=s)
-                        else:
-                            nc.gpsimd.tensor_scalar(out=d, in0=s, scalar1=1.0, scalar2=0.0, op0=ALU.mult, op1=ALU.add)
-                    ops.append(op)
-            return ops
-
-        def quantize_w(grouped, codes, scales, g):
-            nc.vector.quantize_mx(out=codes[:, g, :].bitcast(FP8X4), scales=scales[:, g, :], in_=grouped[:, g, :])
-
-        def new_planes():
-            return stream.tile([P, 8, 512], BF16, name="planes", tag="planes")
-
-        def new_grouped():
-            return const.tile([P, 2, 2048], BF16, name="grouped0", align_bytes=64)
-
-        def new_grouped_half():
-            return stream.tile([P, 1, 2048], BF16, name="grouped", tag="grouped", align_bytes=64, bufs=1)
-
-        def new_codes():
-            wc = stream.tile([P, 2, 512], U32, name="wcodes", tag="wcodes", align_bytes=64)
-            wsl = stream.tile([P, 2, 512], U8, name="wscales", tag="wscales", align_bytes=64)
-            return wc, wsl
-
-        planes_of = {}
-        grouped_of = {}
-        codes_of = {}
-
-        planes_of[0] = new_planes()
-        w0_ops = widen_ops(0, planes_of[0], (6, 7))
-        for gt in (4, 5, 6, 7, 0, 1, 2, 3):
-            w0_ops[gt]()
-
-        ctm = const.tile([P, 2, 8, P], BF16, name="ctm")
-        cs4 = cs[:].rearrange("p i (j e) -> p i j e", e=2)
-        for hh in range(2):
-            d0 = ctm[:, 0, :, 64 * hh : 64 * hh + 64].rearrange("p i (j e) -> p i j e", e=2)
-            nc.gpsimd.tensor_scalar(
-                out=d0, in0=cs4[:, :, :, 0:1].to_broadcast([P, 8, 32, 2]), scalar1=1.0, scalar2=0.0, op0=ALU.mult, op1=ALU.add
-            )
-            d1 = ctm[:, 1, :, 64 * hh : 64 * hh + 64].rearrange("p i (j e) -> p i j e", e=2)
-            for e in range(2):
-                nc.gpsimd.tensor_scalar(
-                    out=d1[:, :, :, e], in0=cs4[:, :, :, 1], scalar1=(1.0 if e == 0 else -1.0), scalar2=0.0,
-                    op0=ALU.mult, op1=ALU.add,
-                )
-
-        grouped_of[0] = new_grouped()
-        codes_of[0] = new_codes()
-        il0 = interleave_ops(0, planes_of[0], grouped_of[0], True)
-        il0[2]()
-        il0[3]()
-        il0[0]()
-        quantize_w(grouped_of[0], codes_of[0][0], codes_of[0][1], 1)
-        il0[1]()
+        for gt in range(8):
+            widen(0, gt, gt in (0, 1))
 
         h_codes = const.tile([P, 2, 1024], U32, name="h_codes", align_bytes=64)
         h_scales = const.tile([P, 2, 1024], U8, name="h_scales", align_bytes=64)
         ct = const.tile([P, 2, 2, 512], BF16, name="ct")
-
-        def hidden_half(q):
+        hgs = []
+        for q in range(2):
             hg = const.tile([P, 2, 4, P, 2], F32, name="hg%d" % q, align_bytes=64)
-            for i4 in range(4):
-                words = xs[q][:, i4, :].bitcast(F32)
-                xt = psum.tile([P, 2, 2, P], F32, name="xt", tag="tr")
-                for g in range(2):
-                    for u in range(2):
-                        nc.tensor.transpose(xt[:, g, u, :], words[:, 256 * g + u : 256 * (g + 1) : 2], ident_f[:])
-                nc.scalar.copy(out=hg[:, :, i4, :, :], in_=xt[:].rearrange("p g u r -> p g r u"))
-            return hg
+            hgs.append(hg)
 
-        def quantize_h(hg, q):
+        def hidden_tile(i):
+            words = xs[i // 2][:, i % 2, :].bitcast(F32)
+            xt = psum.tile([P, 2, 2, P], F32, name="xt", tag="back", bufs=4)
             for g in range(2):
-                nc.vector.quantize_mx(
-                    out=h_codes[:, g, 512 * q : 512 * (q + 1)].bitcast(FP8X4),
-                    scales=h_scales[:, g, 512 * q : 512 * (q + 1)],
-                    in_=hg[:, g].rearrange("p i r u -> p (i r u)").bitcast(BF16),
-                )
+                for u in range(2):
+                    nc.tensor.transpose(xt[:, g, u, :], words[:, 256 * g + u : 256 * (g + 1) : 2], ident_f[:])
+            return xt
+
+        def hidden_copy(xt, i):
+            nc.scalar.copy(out=hgs[i // 4][:, :, i % 4, :, :], in_=xt[:].rearrange("p g u r -> p g r u"))
+
+        def quantize_h(q, g):
+            nc.vector.quantize_mx(
+                out=h_codes[:, g, 512 * q : 512 * (q + 1)].bitcast(FP8X4),
+                scales=h_scales[:, g, 512 * q : 512 * (q + 1)],
+                in_=hgs[q][:, g].rearrange("p i r u -> p (i r u)").bitcast(BF16),
+            )
 
         def table_half(q):
-            ctp = psum.tile([P, 2, 4, P], BF16, name="ctp", tag="tr")
+            ctp = psum.tile([P, 2, 4, P], BF16, name="ctp", tag="pass")
             for tb in range(2):
                 for i4 in range(4):
                     nc.tensor.transpose(ctp[:, tb, i4, :], ctm[:, tb, 4 * q + i4, :], ident_b[:])
+            return ctp
+
+        def table_copy(ctp, q):
             nc.scalar.copy(out=ct[:, q], in_=ctp[:].rearrange("p b i r -> p b (i r)"))
 
-        hg0 = hidden_half(0)
-        quantize_w(grouped_of[0], codes_of[0][0], codes_of[0][1], 0)
-        quantize_h(hg0, 0)
-        table_half(0)
-        planes_of[1] = new_planes()
-        w1_ops = widen_ops(1, planes_of[1], ())
-        for op in w1_ops[0:4]:
-            op()
-        hg1 = hidden_half(1)
-        table_half(1)
-        quantize_h(hg1, 1)
-        for op in w1_ops[4:8]:
-            op()
+        def keep_warm(n):
+            for _ in range(n):
+                wt = psum.tile([P, 512], F32, name="rotb", tag="rot")
+                nc.tensor.matmul(out=wt[:], lhsT=zero[:, 0:P], rhs=zero[:], start=True, stop=True)
+
+        keep_warm(9)
+        xts = []
+        for i in range(2):
+            xts.append(hidden_tile(i))
+        keep_warm(2)
+        for i in range(2, 4):
+            xts.append(hidden_tile(i))
+        keep_warm(2)
+        for i in range(4):
+            hidden_copy(xts[i], i)
+
+        interleave(0, 0, own[:, 0, :], True)
+        quantize_w(0, 0)
+        interleave(0, 1, own[:, 1, :], True)
+        spread_table(0)
+        quantize_w(0, 1)
+        ctp0 = table_half(0)
+        table_copy(ctp0, 0)
+        keep_warm(0)
+        quantize_h(0, 0)
+        quantize_h(0, 1)
+        b_rot = const.tile([P, 9], BF16, name="b_rot")
+        btp = psum.tile([P, P], BF16, name="btp", tag="rot")
+        nc.tensor.transpose(btp[:], bsel[:], ident_b[:])
+        nc.vector.tensor_copy(out=b_rot[:], in_=btp[:, 0:9])
+        spread_table(1)
+        for i in range(4, 6):
+            xts.append(hidden_tile(i))
+        keep_warm(0)
+        for gt in range(2):
+            widen(1, gt, gt < 0)
+        for i in range(4, 6):
+            hidden_copy(xts[i], i)
+        for gt in range(2, 4):
+            widen(1, gt, False)
+        stage_buf = stream.tile([P, 2048], BF16, name="turn", tag="turn", align_bytes=64, bufs=1)
+        interleave(1, 0, stage_buf[:], False)
 
         q_view = out_0.rearrange("o h (p i) c -> p (o h) (i c)", i=8)
         k_view = out_1.rearrange("o h (p i) c -> p (o h) (i c)", i=8)
@@ -250,7 +262,7 @@ def tile_selfattention_pa_kernel(
             return ab
 
         def rot_back(ab):
-            yb = psum.tile([P, 4, P], F32, name="yb", tag="y")
+            yb = psum.tile([P, 4, P], F32, name="yb", tag="back", bufs=4)
             for i4 in range(4):
                 nc.tensor.matmul(out=yb[:, i4, :], lhsT=ab[:, 0, P * i4 : P * (i4 + 1)], rhs=ident_f[:],
                                  is_transpose=True, start=True, stop=False)
@@ -261,10 +273,10 @@ def tile_selfattention_pa_kernel(
         def rot_evac(yb, out_ap):
             nc.scalar.copy(out=out_ap.rearrange("p h i c -> p i h c"), in_=yb[:].rearrange("p i (h c) -> p i h c", c=64))
 
-        def pass_mx(c, col0, width, first_i):
+        def pass_mx(c, col0, width, first_i, tag="pass"):
             wc, wsl = codes_of[c]
             n_i = 512 // width
-            bank = psum.tile([P, n_i, width], F32, name="passb", tag="pass")
+            bank = psum.tile([P, n_i, width], F32, name="passb", tag=tag)
             for ii in range(n_i):
                 i = first_i + ii
                 mx_group(
@@ -295,38 +307,33 @@ def tile_selfattention_pa_kernel(
         b_k = bias_bc[:, 2048:2304].rearrange("p (h f c) -> p f h c", f=2, c=64)[:, 1]
         b_v = bias_bc[:, 2304:2560].rearrange("p (h c) -> p h c", c=128)
 
-        il_of = {}
-
-        def prep_widen(c, g):
-            if g == 0:
-                planes_of[c] = new_planes()
-            for op in widen_ops(c, planes_of[c], ())[4 * g : 4 * g + 4]:
-                op()
-
-        def prep_interleave(c, g):
-            il_of[(c, g)] = new_grouped_half()
-            for op in interleave_ops(c, planes_of[c], il_of[(c, g)], False, (g,)):
-                op()
-
-        def prep_quantize(c, g):
-            if g == 0:
-                codes_of[c] = new_codes()
-            nc.vector.quantize_mx(
-                out=codes_of[c][0][:, g, :].bitcast(FP8X4), scales=codes_of[c][1][:, g, :], in_=il_of[(c, g)][:, 0, :]
-            )
-
-        prep_interleave(1, 0)
-
-        ctx.enter_context(tc.manual_schedule())
         prev = None
         for k in range(len(slots)):
             sl = slots[k]
             c = sl["c"]
-            for cw in range(2, 5):
-                for g in range(2):
-                    if 2 * cw - 4 + g == k:
-                        prep_widen(cw, g)
             banks = [rot_mx(*u) for u in sl["ropes"]]
+            if k == 0:
+                for i in range(6, 8):
+                    xts.append(hidden_tile(i))
+                for i in range(6, 8):
+                    hidden_copy(xts[i], i)
+            if 0 < k < 6:
+                for t in range(4):
+                    widen(2 + k // 2, 4 * (k % 2) + t, False)
+            if prev is not None and prev["ropes"]:
+                ybs = [rot_back(ab) for ab in prev["abs"]]
+                pres = prev["res"]
+                flat = pres[:].rearrange("p h i c -> p h (i c)")
+                for j in range(len(ybs)):
+                    if prev["kind"] == "q":
+                        rot_evac(ybs[j], pres[:, 2 * j : 2 * j + 2, :, 0:64])
+                    else:
+                        rot_evac(ybs[j], pres[:, :, 4 * j : 4 * j + 4, 0:64])
+                        nc.sync.dma_start(out=k_view[:, :, 512 * j : 512 * (j + 1)], in_=flat[:, :, 512 * j : 512 * (j + 1)])
+                if prev["kind"] == "q":
+                    pc = prev["c"]
+                    pq = prev["q"]
+                    nc.sync.dma_start(out=q_view[:, 4 * pc : 4 * pc + 4, 512 * pq : 512 * (pq + 1)], in_=flat)
             adds = []
             if sl["kind"] == "q":
                 q = sl["q"]
@@ -342,30 +349,27 @@ def tile_selfattention_pa_kernel(
             else:
                 res = new_res([P, 2, 8, P])
                 sl["res"] = res
-                for ip in range(2):
-                    adds.append((pass_mx(4, 256, 256, 2 * ip), res[:, :, 2 * ip : 2 * ip + 2, :], b_v))
-            if prev is not None and prev["ropes"]:
-                ybs = [rot_back(ab) for ab in prev["abs"]]
-                pres = prev["res"]
-                flat = pres[:].rearrange("p h i c -> p h (i c)")
-                for j in range(len(ybs)):
-                    if prev["kind"] == "q":
-                        rot_evac(ybs[j], pres[:, 2 * j : 2 * j + 2, :, 0:64])
-                    else:
-                        rot_evac(ybs[j], pres[:, :, 4 * j : 4 * j + 4, 0:64])
-                        nc.sync.dma_start(out=k_view[:, :, 512 * j : 512 * (j + 1)], in_=flat[:, :, 512 * j : 512 * (j + 1)])
-                if prev["kind"] == "q":
-                    pc = prev["c"]
-                    pq = prev["q"]
-                    nc.sync.dma_start(out=q_view[:, 4 * pc : 4 * pc + 4, 512 * pq : 512 * (pq + 1)], in_=flat)
-            if sl["kind"] == "v":
-                for ip in range(2, 4):
-                    adds.append((pass_mx(4, 256, 256, 2 * ip), res[:, :, 2 * ip : 2 * ip + 2, :], b_v))
+                for ip in range(4):
+                    tag = "pass" if ip < 2 else "rot"
+                    adds.append((pass_mx(4, 256, 256, 2 * ip, tag), res[:, :, 2 * ip : 2 * ip + 2, :], b_v))
+            if k == 0:
+                table_copy(table_half(1), 1)
+                for gt in range(4, 8):
+                    widen(1, gt, False)
+                for gt in range(4):
+                    widen(2, gt, False)
             sl["abs"] = [rot_mul(banks[j], *sl["ropes"][j]) for j in range(len(banks))]
+            if k == 0:
+                for bank, out_ap, bias_ap in adds:
+                    pass_add(bank, out_ap, bias_ap)
+                adds = []
+                quantize_h(1, 0)
+                quantize_h(1, 1)
             if k < 8:
-                prep_quantize(1 + k // 2, k % 2)
+                quantize_w(1 + k // 2, k % 2)
             if k < 7:
-                prep_interleave(1 + (k + 1) // 2, (k + 1) % 2)
+                stage_buf = stream.tile([P, 2048], BF16, name="turn", tag="turn", align_bytes=64, bufs=1)
+                interleave(1 + (k + 1) // 2, (k + 1) % 2, stage_buf[:], False)
             n_add = 0
             for bank, out_ap, bias_ap in adds:
                 pass_add(bank, out_ap, bias_ap)

@@ -35,6 +35,8 @@ def tile_selfattention_pa_kernel(
         nc.vector.memset(warm[:, 0:1], 0.0)
         nc.scalar.activation(out=warm[:, 1:2], in_=warm[:, 0:1], func=ACT.Copy)
 
+        cs = const.tile([P, 8, 64], BF16, name="cs")
+        nc.sync.dma_start(out=cs[:], in_=rope_cache.rearrange("o (p i) j e -> (o p) i (j e)", i=8))
         wsc = const.tile([P, 8], F32, name="wsc")
         nc.sync.dma_start(
             out=wsc[:].rearrange("p (g t) -> p g t", g=2),
@@ -60,8 +62,6 @@ def tile_selfattention_pa_kernel(
 
         load_w(0)
         load_x(0)
-        cs = const.tile([P, 8, 64], BF16, name="cs")
-        nc.sync.dma_start(out=cs[:], in_=rope_cache.rearrange("o (p i) j e -> (o p) i (j e)", i=8))
         load_x(1)
         nc.sync.dma_start(
             out=bsel[0:9, :].rearrange("r (hh c) -> r hh c", hh=2),
@@ -76,10 +76,10 @@ def tile_selfattention_pa_kernel(
         load_w(3)
         load_w(4)
 
-        ident_f = const.tile([P, P], F32, name="ident_f")
-        make_identity(nc, ident_f[:])
         ident_b = const.tile([P, P], BF16, name="ident_b")
         make_identity(nc, ident_b[:])
+        ident_f = const.tile([P, P], F32, name="ident_f")
+        make_identity(nc, ident_f[:])
 
         planes_of = {}
         grouped_of = {}
@@ -125,27 +125,42 @@ def tile_selfattention_pa_kernel(
 
         own = const.tile([P, 2, 2048], BF16, name="own", align_bytes=64)
 
-        ctm = const.tile([P, 2, 8, P], BF16, name="ctm")
-        cs4 = cs[:].rearrange("p i (j e) -> p i j e", e=2)
-        def spread_table(q):
-            rows = slice(4 * q, 4 * q + 4)
-            for hh in range(2):
-                nc.vector.tensor_scalar(
-                    out=ctm[:, 0, rows, 64 * hh : 64 * hh + 64].rearrange("p i (j e) -> p i j e", e=2),
-                    in0=cs4[:, rows, :, 0:1].to_broadcast([P, 4, 32, 2]), scalar1=1.0, scalar2=0.0, op0=ALU.mult, op1=ALU.add,
-                )
-            dst = ctm[:, 1, rows, :].rearrange("p i (hh j e) -> p e i hh j", hh=2, e=2)
+        pick = const.tile([P, 2, 2, P], BF16, name="pick")
+        id4 = ident_b[:].rearrange("p (i2 j e) -> p i2 j e", i2=2, e=2)
+        for s in range(2):
+            nc.gpsimd.tensor_scalar(
+                out=pick[:, 0, s, :].rearrange("p (hh j e) -> p hh j e", hh=2, e=2),
+                in0=id4[:, s, :, 0].unsqueeze(1).unsqueeze(3).to_broadcast([P, 2, 32, 2]),
+                scalar1=1.0, scalar2=0.0, op0=ALU.mult, op1=ALU.add,
+            )
             for e in range(2):
-                nc.vector.tensor_scalar(
-                    out=dst[:, e], in0=cs4[:, rows, :, 1].unsqueeze(2).to_broadcast([P, 4, 2, 32]),
+                nc.gpsimd.tensor_scalar(
+                    out=pick[:, 1, s, :].rearrange("p (hh j e) -> p e hh j", hh=2, e=2)[:, e],
+                    in0=id4[:, s, :, 1].unsqueeze(1).to_broadcast([P, 2, 32]),
                     scalar1=(1.0 if e == 0 else -1.0), scalar2=0.0, op0=ALU.mult, op1=ALU.add,
                 )
-
         perm_f = const.tile([P, P], F32, name="perm_f")
         id_pairs = ident_f[:].rearrange("p (m e) -> p m e", e=2)
         pm_pairs = perm_f[:].rearrange("p (m e) -> p m e", e=2)
         nc.gpsimd.tensor_copy(out=pm_pairs[:, :, 0], in_=id_pairs[:, :, 1])
         nc.gpsimd.tensor_copy(out=pm_pairs[:, :, 1], in_=id_pairs[:, :, 0])
+
+        csT = const.tile([P, 4, P], BF16, name="csT")
+
+        def keep_warm(n):
+            for _ in range(n):
+                wt = psum.tile([P, 512], F32, name="rotb", tag="rot")
+                nc.tensor.matmul(out=wt[:], lhsT=zero[:, 0:P], rhs=zero[:], start=True, stop=True)
+
+        def turn_cache():
+            cp = psum.tile([P, 4, P], BF16, name="cp", tag="pass")
+            for s2 in range(4):
+                nc.tensor.transpose(cp[:, s2, :], cs[:, 2 * s2 : 2 * s2 + 2, :].rearrange("p i c -> p (i c)"), ident_b[:])
+            nc.scalar.copy(out=csT[:], in_=cp[:])
+
+        keep_warm(5)
+        turn_cache()
+        keep_warm(6)
 
         for gt in range(8):
             widen(0, gt, gt in (0, 1))
@@ -177,21 +192,15 @@ def tile_selfattention_pa_kernel(
             )
 
         def table_half(q):
-            ctp = psum.tile([P, 2, 4, P], BF16, name="ctp", tag="pass")
+            ctp = psum.tile([P, 2, 4, P], BF16, name="ctp", tag=("pass" if q == 0 else "rot"))
             for tb in range(2):
                 for i4 in range(4):
-                    nc.tensor.transpose(ctp[:, tb, i4, :], ctm[:, tb, 4 * q + i4, :], ident_b[:])
+                    nc.tensor.matmul(out=ctp[:, tb, i4, :], lhsT=pick[:, tb, i4 % 2, :], rhs=csT[:, 2 * q + i4 // 2, :], start=True, stop=True)
             return ctp
 
         def table_copy(ctp, q):
             nc.scalar.copy(out=ct[:, q], in_=ctp[:].rearrange("p b i r -> p b (i r)"))
 
-        def keep_warm(n):
-            for _ in range(n):
-                wt = psum.tile([P, 512], F32, name="rotb", tag="rot")
-                nc.tensor.matmul(out=wt[:], lhsT=zero[:, 0:P], rhs=zero[:], start=True, stop=True)
-
-        keep_warm(9)
         xts = []
         for i in range(2):
             xts.append(hidden_tile(i))
@@ -205,7 +214,6 @@ def tile_selfattention_pa_kernel(
         interleave(0, 0, own[:, 0, :], True)
         quantize_w(0, 0)
         interleave(0, 1, own[:, 1, :], True)
-        spread_table(0)
         quantize_w(0, 1)
         ctp0 = table_half(0)
         table_copy(ctp0, 0)
@@ -216,18 +224,13 @@ def tile_selfattention_pa_kernel(
         btp = psum.tile([P, P], BF16, name="btp", tag="rot")
         nc.tensor.transpose(btp[:], bsel[:], ident_b[:])
         nc.vector.tensor_copy(out=b_rot[:], in_=btp[:, 0:9])
-        spread_table(1)
         for i in range(4, 6):
             xts.append(hidden_tile(i))
         keep_warm(0)
-        for gt in range(2):
+        for gt in range(4):
             widen(1, gt, gt < 0)
         for i in range(4, 6):
             hidden_copy(xts[i], i)
-        for gt in range(2, 4):
-            widen(1, gt, False)
-        stage_buf = stream.tile([P, 2048], BF16, name="turn", tag="turn", align_bytes=64, bufs=1)
-        interleave(1, 0, stage_buf[:], False)
 
         q_view = out_0.rearrange("o h (p i) c -> p (o h) (i c)", i=8)
         k_view = out_1.rearrange("o h (p i) c -> p (o h) (i c)", i=8)
@@ -312,11 +315,6 @@ def tile_selfattention_pa_kernel(
             sl = slots[k]
             c = sl["c"]
             banks = [rot_mx(*u) for u in sl["ropes"]]
-            if k == 0:
-                for i in range(6, 8):
-                    xts.append(hidden_tile(i))
-                for i in range(6, 8):
-                    hidden_copy(xts[i], i)
             if 0 < k < 6:
                 for t in range(4):
                     widen(2 + k // 2, 4 * (k % 2) + t, False)
@@ -327,13 +325,12 @@ def tile_selfattention_pa_kernel(
                 for j in range(len(ybs)):
                     if prev["kind"] == "q":
                         rot_evac(ybs[j], pres[:, 2 * j : 2 * j + 2, :, 0:64])
+                        pc = prev["c"]
+                        pq = prev["q"]
+                        nc.sync.dma_start(out=q_view[:, 4 * pc + 2 * j : 4 * pc + 2 * j + 2, 512 * pq : 512 * (pq + 1)], in_=flat[:, 2 * j : 2 * j + 2])
                     else:
                         rot_evac(ybs[j], pres[:, :, 4 * j : 4 * j + 4, 0:64])
                         nc.sync.dma_start(out=k_view[:, :, 512 * j : 512 * (j + 1)], in_=flat[:, :, 512 * j : 512 * (j + 1)])
-                if prev["kind"] == "q":
-                    pc = prev["c"]
-                    pq = prev["q"]
-                    nc.sync.dma_start(out=q_view[:, 4 * pc : 4 * pc + 4, 512 * pq : 512 * (pq + 1)], in_=flat)
             adds = []
             if sl["kind"] == "q":
                 q = sl["q"]
@@ -353,7 +350,12 @@ def tile_selfattention_pa_kernel(
                     tag = "pass" if ip < 2 else "rot"
                     adds.append((pass_mx(4, 256, 256, 2 * ip, tag), res[:, :, 2 * ip : 2 * ip + 2, :], b_v))
             if k == 0:
-                table_copy(table_half(1), 1)
+                ctp1 = table_half(1)
+                for i in range(6, 8):
+                    xts.append(hidden_tile(i))
+                table_copy(ctp1, 1)
+                for i in range(6, 8):
+                    hidden_copy(xts[i], i)
                 for gt in range(4, 8):
                     widen(1, gt, False)
                 for gt in range(4):
@@ -363,6 +365,7 @@ def tile_selfattention_pa_kernel(
                 for bank, out_ap, bias_ap in adds:
                     pass_add(bank, out_ap, bias_ap)
                 adds = []
+                interleave(1, 0, own[:, 0, :], True)
                 quantize_h(1, 0)
                 quantize_h(1, 1)
             if k < 8:

@@ -44,13 +44,13 @@ def tile_selfattention_pa_kernel(
         )
 
         w_view = w_qkv_bytes.rearrange("(g p t) n -> g p t n", p=P, t=4)
-        wb = []
+        wb = {}
 
         def load_w(c):
             t = const.tile([P, 8, 512], U8, name="wbytes%d" % c)
             for g in range(2):
                 nc.sync.dma_start(out=t[:, 4 * g : 4 * g + 4, :], in_=w_view[g, :, :, 512 * c : 512 * (c + 1)])
-            wb.append(t)
+            wb[c] = t
 
         x_view = hidden_states.rearrange("o (p i) k -> (o p) i k", i=8)
         xs = []
@@ -72,9 +72,8 @@ def tile_selfattention_pa_kernel(
         load_w(1)
         bias_bc = const.tile([P, 2560], BF16, name="bias_bc")
         nc.sync.dma_start(out=bias_bc[:], in_=b_qkv.partition_broadcast(P))
-        load_w(2)
-        load_w(3)
-        load_w(4)
+        for c in (0, 1, 2, 3, 4)[2:]:
+            load_w(c)
 
         ident_b = const.tile([P, P], BF16, name="ident_b")
         make_identity(nc, ident_b[:])
@@ -95,7 +94,7 @@ def tile_selfattention_pa_kernel(
             else:
                 nc.scalar.activation(out=dst, in_=src, func=ACT.Copy, scale=wsc[:, gt : gt + 1])
 
-        def interleave(c, g, dst, on_vector):
+        def interleave(c, g, dst, engine, parts=(0, 1, 2)):
             grouped_of[(c, g)] = dst
             src = planes_of[c][:, 4 * g : 4 * g + 4, :]
             pairs = []
@@ -108,16 +107,20 @@ def tile_selfattention_pa_kernel(
                 for f in range(2):
                     pairs.append((dst[:, 512 * f : 512 * (f + 1)].rearrange("p (h c t) -> p h c t", h=2, t=4), sv[:, f]))
                 pairs.append((dst[:, 1024:2048].rearrange("p (n t) -> p n t", t=4), src[:, :, 256:512].rearrange("p t n -> p n t")))
-            for d, s in pairs:
-                if on_vector:
+            for n, (d, s) in enumerate(pairs):
+                if n not in parts:
+                    continue
+                if engine == "vector":
                     nc.vector.tensor_copy(out=d, in_=s)
+                elif engine == "scalar":
+                    nc.scalar.copy(out=d, in_=s)
                 else:
                     nc.gpsimd.tensor_scalar(out=d, in0=s, scalar1=1.0, scalar2=0.0, op0=ALU.mult, op1=ALU.add)
 
         def quantize_w(c, g):
             if c not in codes_of:
-                wc = stream.tile([P, 2, 512], U32, name="wcodes", tag="wcodes", align_bytes=64, bufs=3)
-                wsl = stream.tile([P, 2, 512], U8, name="wscales", tag="wscales", align_bytes=64, bufs=3)
+                wc = stream.tile([P, 2, 512], U32, name="wcodes", tag="wcodes", align_bytes=64, bufs=5)
+                wsl = stream.tile([P, 2, 512], U8, name="wscales", tag="wscales", align_bytes=64, bufs=5)
                 codes_of[c] = (wc, wsl)
             nc.vector.quantize_mx(
                 out=codes_of[c][0][:, g, :].bitcast(FP8X4), scales=codes_of[c][1][:, g, :], in_=grouped_of[(c, g)]
@@ -211,9 +214,9 @@ def tile_selfattention_pa_kernel(
         for i in range(4):
             hidden_copy(xts[i], i)
 
-        interleave(0, 0, own[:, 0, :], True)
+        interleave(0, 0, own[:, 0, :], "vector")
         quantize_w(0, 0)
-        interleave(0, 1, own[:, 1, :], True)
+        interleave(0, 1, own[:, 1, :], "vector")
         quantize_w(0, 1)
         ctp0 = table_half(0)
         table_copy(ctp0, 0)
@@ -229,6 +232,8 @@ def tile_selfattention_pa_kernel(
         keep_warm(0)
         for gt in range(4):
             widen(1, gt, gt < 0)
+        stage_buf = stream.tile([P, 2048], BF16, name="turn", tag="turn", align_bytes=64, bufs=1)
+        interleave(1, 0, stage_buf[:], "gpsimd")
         for i in range(4, 6):
             hidden_copy(xts[i], i)
 
@@ -298,26 +303,25 @@ def tile_selfattention_pa_kernel(
             )
 
         def new_res(shape):
-            return stream.tile(shape, F32, name="res", tag="res", bufs=4)
+            return stream.tile(shape, F32, name="res", tag="res", bufs=10)
 
         slots = []
-        for c in range(4):
+        def add_q(c):
             b_ap = bias_bc[:, 512 * c : 512 * (c + 1)].rearrange("p (h f c) -> p f h c", f=2, c=64)[:, 1]
             for q in range(2):
                 slots.append({"c": c, "q": q, "ropes": [(c, 0, q), (c, 1, q)], "kind": "q", "bias": b_ap})
-        slots.append({"c": 4, "kind": "k", "ropes": [(4, 0, 0), (4, 0, 1)]})
-        slots.append({"c": 4, "kind": "v", "ropes": []})
+
+        for c in (0, 1, 2, 3, 4):
+            if c < 4:
+                add_q(c)
+            else:
+                slots.append({"c": 4, "kind": "k", "ropes": [(4, 0, 0), (4, 0, 1)]})
+                slots.append({"c": 4, "kind": "v", "ropes": []})
+        order = (0, 1, 2, 3, 4)
         b_k = bias_bc[:, 2048:2304].rearrange("p (h f c) -> p f h c", f=2, c=64)[:, 1]
         b_v = bias_bc[:, 2304:2560].rearrange("p (h c) -> p h c", c=128)
 
-        prev = None
-        for k in range(len(slots)):
-            sl = slots[k]
-            c = sl["c"]
-            banks = [rot_mx(*u) for u in sl["ropes"]]
-            if 0 < k < 6:
-                for t in range(4):
-                    widen(2 + k // 2, 4 * (k % 2) + t, False)
+        def turn_back(prev):
             if prev is not None and prev["ropes"]:
                 ybs = [rot_back(ab) for ab in prev["abs"]]
                 pres = prev["res"]
@@ -331,6 +335,16 @@ def tile_selfattention_pa_kernel(
                     else:
                         rot_evac(ybs[j], pres[:, :, 4 * j : 4 * j + 4, 0:64])
                         nc.sync.dma_start(out=k_view[:, :, 512 * j : 512 * (j + 1)], in_=flat[:, :, 512 * j : 512 * (j + 1)])
+
+        prev = None
+        for k in range(len(slots)):
+            sl = slots[k]
+            c = sl["c"]
+            banks = [rot_mx(*u) for u in sl["ropes"]]
+            if 0 < k < 6:
+                for t in range(4):
+                    widen(order[2 + k // 2], 4 * (k % 2) + t, False)
+            turn_back(prev)
             adds = []
             if sl["kind"] == "q":
                 q = sl["q"]
@@ -365,14 +379,16 @@ def tile_selfattention_pa_kernel(
                 for bank, out_ap, bias_ap in adds:
                     pass_add(bank, out_ap, bias_ap)
                 adds = []
-                interleave(1, 0, own[:, 0, :], True)
                 quantize_h(1, 0)
                 quantize_h(1, 1)
             if k < 8:
-                quantize_w(1 + k // 2, k % 2)
+                quantize_w(order[1 + k // 2], k % 2)
             if k < 7:
                 stage_buf = stream.tile([P, 2048], BF16, name="turn", tag="turn", align_bytes=64, bufs=1)
-                interleave(1 + (k + 1) // 2, (k + 1) % 2, stage_buf[:], False)
+                n_s = (0, 0, 0, 0, 0, 0, 3, 3)[k + 1]
+                cn = order[1 + (k + 1) // 2]
+                n_parts = 2 if cn < 4 else 3
+                interleave(cn, (k + 1) % 2, stage_buf[:], "gpsimd", range(0, n_parts - n_s))
             n_add = 0
             for bank, out_ap, bias_ap in adds:
                 pass_add(bank, out_ap, bias_ap)
@@ -382,4 +398,7 @@ def tile_selfattention_pa_kernel(
                         in_=res[:].rearrange("p h i c -> p h (i c)")[:, :, 256 * n_add : 256 * (n_add + 1)],
                     )
                 n_add += 1
+            if k < 7:
+                interleave(cn, (k + 1) % 2, stage_buf[:], "scalar", range(n_parts - n_s, n_parts))
             prev = sl
+        turn_back(prev)

@@ -98,7 +98,9 @@ def tile_selfattention_pa_kernel(
             grouped_of[(c, g)] = dst
             src = planes_of[c][:, 4 * g : 4 * g + 4, :]
             pairs = []
-            if c < 4:
+            if c < 4 and engine == "vector":
+                pairs.append((dst.rearrange("p (f h c t) -> p f h c t", f=2, h=4, t=4), src.rearrange("p t (h f c) -> p f h c t", f=2, c=64)))
+            elif c < 4:
                 sv = src.rearrange("p t (h f c) -> p f h c t", f=2, c=64)
                 for f in range(2):
                     pairs.append((dst[:, 1024 * f : 1024 * (f + 1)].rearrange("p (h c t) -> p h c t", h=4, t=4), sv[:, f]))
@@ -150,9 +152,9 @@ def tile_selfattention_pa_kernel(
 
         csT = const.tile([P, 4, P], BF16, name="csT")
 
-        def keep_warm(n):
+        def keep_warm(n, tag="rot", bufs=2):
             for _ in range(n):
-                wt = psum.tile([P, 512], F32, name="rotb", tag="rot")
+                wt = psum.tile([P, 512], F32, name="wt", tag=tag, bufs=bufs)
                 nc.tensor.matmul(out=wt[:], lhsT=zero[:, 0:P], rhs=zero[:], start=True, stop=True)
 
         def turn_cache():
@@ -166,7 +168,7 @@ def tile_selfattention_pa_kernel(
         keep_warm(6)
 
         for gt in range(8):
-            widen(0, gt, gt in (0, 1))
+            widen(0, gt, gt in (0, 1, 4))
 
         h_codes = const.tile([P, 2, 1024], U32, name="h_codes", align_bytes=64)
         h_scales = const.tile([P, 2, 1024], U8, name="h_scales", align_bytes=64)
@@ -231,7 +233,7 @@ def tile_selfattention_pa_kernel(
             xts.append(hidden_tile(i))
         keep_warm(0)
         for gt in range(4):
-            widen(1, gt, gt < 0)
+            widen(1, gt, gt < 1)
         stage_buf = stream.tile([P, 2048], BF16, name="turn", tag="turn", align_bytes=64, bufs=1)
         interleave(1, 0, stage_buf[:], "gpsimd")
         for i in range(4, 6):
@@ -340,11 +342,14 @@ def tile_selfattention_pa_kernel(
         for k in range(len(slots)):
             sl = slots[k]
             c = sl["c"]
+            if k >= 8:
+                turn_back(prev)
             banks = [rot_mx(*u) for u in sl["ropes"]]
             if 0 < k < 6:
                 for t in range(4):
                     widen(order[2 + k // 2], 4 * (k % 2) + t, False)
-            turn_back(prev)
+            if k < 8:
+                turn_back(prev)
             adds = []
             if sl["kind"] == "q":
                 q = sl["q"]
@@ -367,10 +372,11 @@ def tile_selfattention_pa_kernel(
                 ctp1 = table_half(1)
                 for i in range(6, 8):
                     xts.append(hidden_tile(i))
+                keep_warm(3, "back", 4)
                 table_copy(ctp1, 1)
                 for i in range(6, 8):
                     hidden_copy(xts[i], i)
-                for gt in range(4, 8):
+                for gt in range(4, 8 - 1):
                     widen(1, gt, False)
                 for gt in range(4):
                     widen(2, gt, False)
@@ -379,13 +385,16 @@ def tile_selfattention_pa_kernel(
                 for bank, out_ap, bias_ap in adds:
                     pass_add(bank, out_ap, bias_ap)
                 adds = []
+                quantize_w(order[1], 0)
                 quantize_h(1, 0)
                 quantize_h(1, 1)
-            if k < 8:
+                for gt in range(8 - 1, 8):
+                    widen(1, gt, True)
+            if 0 < k < 8:
                 quantize_w(order[1 + k // 2], k % 2)
             if k < 7:
                 stage_buf = stream.tile([P, 2048], BF16, name="turn", tag="turn", align_bytes=64, bufs=1)
-                n_s = (0, 0, 0, 0, 0, 0, 3, 3)[k + 1]
+                n_s = (0,0,0,0,0,0,3,3)[k + 1]
                 cn = order[1 + (k + 1) // 2]
                 n_parts = 2 if cn < 4 else 3
                 interleave(cn, (k + 1) % 2, stage_buf[:], "gpsimd", range(0, n_parts - n_s))

@@ -46,11 +46,17 @@ def tile_selfattention_pa_kernel(
         w_view = w_qkv_bytes.rearrange("(g p t) n -> g p t n", p=P, t=4)
         wb = {}
 
-        def load_w(c):
-            t = const.tile([P, 8, 512], U8, name="wbytes%d" % c)
-            for g in range(2):
-                nc.sync.dma_start(out=t[:, 4 * g : 4 * g + 4, :], in_=w_view[g, :, :, 512 * c : 512 * (c + 1)])
-            wb[c] = t
+        for c in range(5):
+            wt = const.tile([P, 8, 512], U8, name="wbytes%d" % c)
+            wb[c] = wt
+
+        def load_w(c, g):
+            cols = slice(512 * c, 512 * (c + 1))
+            if c == 0 and g == 0:
+                for e in range(2):
+                    nc.sync.dma_start(out=wb[c][:, e:4:2, :], in_=w_view[g, :, e:4:2, cols])
+            else:
+                nc.sync.dma_start(out=wb[c][:, 4 * g : 4 * g + 4, :], in_=w_view[g, :, :, cols])
 
         x_view = hidden_states.rearrange("o (p i) k -> (o p) i k", i=8)
         xs = []
@@ -60,7 +66,8 @@ def tile_selfattention_pa_kernel(
             nc.sync.dma_start(out=t[:], in_=x_view[:, 2 * h : 2 * h + 2, :])
             xs.append(t)
 
-        load_w(0)
+        load_w(0, 0)
+        load_w(0, 1)
         load_x(0)
         load_x(1)
         nc.sync.dma_start(
@@ -68,12 +75,14 @@ def tile_selfattention_pa_kernel(
             in_=b_qkv[0:2304].rearrange("(r hh f c) -> r hh f c", hh=2, f=2, c=64)[:, :, 0, :],
         )
         load_x(2)
+        load_w(1, 0)
         load_x(3)
-        load_w(1)
+        load_w(1, 1)
         bias_bc = const.tile([P, 2560], BF16, name="bias_bc")
         nc.sync.dma_start(out=bias_bc[:], in_=b_qkv.partition_broadcast(P))
         for c in (0, 1, 2, 3, 4)[2:]:
-            load_w(c)
+            for g in range(2):
+                load_w(c, g)
 
         ident_b = const.tile([P, P], BF16, name="ident_b")
         make_identity(nc, ident_b[:])
@@ -97,18 +106,26 @@ def tile_selfattention_pa_kernel(
         def interleave(c, g, dst, engine, parts=(0, 1, 2)):
             grouped_of[(c, g)] = dst
             src = planes_of[c][:, 4 * g : 4 * g + 4, :]
+            nh = 4 if c < 4 else 2
+            w = 256 * nh
+            sv = src[:, :, 0 : 128 * nh]
             pairs = []
-            if c < 4 and engine == "vector":
-                pairs.append((dst.rearrange("p (f h c t) -> p f h c t", f=2, h=4, t=4), src.rearrange("p t (h f c) -> p f h c t", f=2, c=64)))
-            elif c < 4:
-                sv = src.rearrange("p t (h f c) -> p f h c t", f=2, c=64)
-                for f in range(2):
-                    pairs.append((dst[:, 1024 * f : 1024 * (f + 1)].rearrange("p (h c t) -> p h c t", h=4, t=4), sv[:, f]))
-            else:
-                sv = src[:, :, 0:256].rearrange("p t (h f c) -> p f h c t", f=2, c=64)
-                for f in range(2):
-                    pairs.append((dst[:, 512 * f : 512 * (f + 1)].rearrange("p (h c t) -> p h c t", h=2, t=4), sv[:, f]))
-                pairs.append((dst[:, 1024:2048].rearrange("p (n t) -> p n t", t=4), src[:, :, 256:512].rearrange("p t n -> p n t")))
+            for f in range(2):
+                if engine == "gpsimd":
+                    pairs.append((
+                        dst[:, w * f : w * (f + 1)].rearrange("p (h c t) -> p h c t", h=nh, t=4),
+                        sv.rearrange("p t (h f c) -> p f h c t", f=2, c=64)[:, f],
+                    ))
+                else:
+                    pairs.append((
+                        dst[:, w * f : w * (f + 1)].rearrange("p (h c i t) -> p h c t i", h=nh, i=4, t=4),
+                        sv.rearrange("p t (h f c i) -> p f h c t i", f=2, c=16, i=4)[:, f],
+                    ))
+            if c == 4:
+                if engine == "gpsimd":
+                    pairs.append((dst[:, 1024:2048].rearrange("p (n t) -> p n t", t=4), src[:, :, 256:512].rearrange("p t n -> p n t")))
+                else:
+                    pairs.append((dst[:, 1024:2048].rearrange("p (n i t) -> p n t i", i=4, t=4), src[:, :, 256:512].rearrange("p t (n i) -> p n t i", i=4)))
             for n, (d, s) in enumerate(pairs):
                 if n not in parts:
                     continue
@@ -161,14 +178,13 @@ def tile_selfattention_pa_kernel(
             cp = psum.tile([P, 4, P], BF16, name="cp", tag="pass")
             for s2 in range(4):
                 nc.tensor.transpose(cp[:, s2, :], cs[:, 2 * s2 : 2 * s2 + 2, :].rearrange("p i c -> p (i c)"), ident_b[:])
-            nc.scalar.copy(out=csT[:], in_=cp[:])
+            nc.vector.tensor_copy(out=csT[:], in_=cp[:])
 
         keep_warm(5)
-        turn_cache()
-        keep_warm(6)
-
         for gt in range(8):
             widen(0, gt, gt in (0, 1, 4))
+        turn_cache()
+        keep_warm(6)
 
         h_codes = const.tile([P, 2, 1024], U32, name="h_codes", align_bytes=64)
         h_scales = const.tile([P, 2, 1024], U8, name="h_scales", align_bytes=64)
@@ -221,6 +237,8 @@ def tile_selfattention_pa_kernel(
         interleave(0, 1, own[:, 1, :], "vector")
         quantize_w(0, 1)
         ctp0 = table_half(0)
+        for gt in range(1, 1 + 1):
+            widen(1, gt, False)
         table_copy(ctp0, 0)
         keep_warm(0)
         quantize_h(0, 0)
@@ -232,12 +250,15 @@ def tile_selfattention_pa_kernel(
         for i in range(4, 6):
             xts.append(hidden_tile(i))
         keep_warm(0)
-        for gt in range(4):
-            widen(1, gt, gt < 1)
+        for gt in range(1):
+            widen(1, gt, True)
+        for gt in range(1 + 1, 4):
+            widen(1, gt, False)
         stage_buf = stream.tile([P, 2048], BF16, name="turn", tag="turn", align_bytes=64, bufs=1)
         interleave(1, 0, stage_buf[:], "gpsimd")
         for i in range(4, 6):
             hidden_copy(xts[i], i)
+        widen(1, 4, False)
 
         q_view = out_0.rearrange("o h (p i) c -> p (o h) (i c)", i=8)
         k_view = out_1.rearrange("o h (p i) c -> p (o h) (i c)", i=8)
@@ -373,10 +394,10 @@ def tile_selfattention_pa_kernel(
                 for i in range(6, 8):
                     xts.append(hidden_tile(i))
                 keep_warm(3, "back", 4)
-                table_copy(ctp1, 1)
                 for i in range(6, 8):
                     hidden_copy(xts[i], i)
-                for gt in range(4, 8 - 1):
+                table_copy(ctp1, 1)
+                for gt in range(5, 8 - 1):
                     widen(1, gt, False)
                 for gt in range(4):
                     widen(2, gt, False)
@@ -385,11 +406,15 @@ def tile_selfattention_pa_kernel(
                 for bank, out_ap, bias_ap in adds:
                     pass_add(bank, out_ap, bias_ap)
                 adds = []
+                if 1:
+                    for gt in range(8 - 1, 8):
+                        widen(1, gt, True)
                 quantize_w(order[1], 0)
                 quantize_h(1, 0)
                 quantize_h(1, 1)
-                for gt in range(8 - 1, 8):
-                    widen(1, gt, True)
+                if not 1:
+                    for gt in range(8 - 1, 8):
+                        widen(1, gt, True)
             if 0 < k < 8:
                 quantize_w(order[1 + k // 2], k % 2)
             if k < 7:

@@ -106,26 +106,18 @@ def tile_selfattention_pa_kernel(
         def interleave(c, g, dst, engine, parts=(0, 1, 2)):
             grouped_of[(c, g)] = dst
             src = planes_of[c][:, 4 * g : 4 * g + 4, :]
-            nh = 4 if c < 4 else 2
-            w = 256 * nh
-            sv = src[:, :, 0 : 128 * nh]
             pairs = []
-            for f in range(2):
-                if engine == "gpsimd":
-                    pairs.append((
-                        dst[:, w * f : w * (f + 1)].rearrange("p (h c t) -> p h c t", h=nh, t=4),
-                        sv.rearrange("p t (h f c) -> p f h c t", f=2, c=64)[:, f],
-                    ))
-                else:
-                    pairs.append((
-                        dst[:, w * f : w * (f + 1)].rearrange("p (h c i t) -> p h c t i", h=nh, i=4, t=4),
-                        sv.rearrange("p t (h f c i) -> p f h c t i", f=2, c=16, i=4)[:, f],
-                    ))
-            if c == 4:
-                if engine == "gpsimd":
-                    pairs.append((dst[:, 1024:2048].rearrange("p (n t) -> p n t", t=4), src[:, :, 256:512].rearrange("p t n -> p n t")))
-                else:
-                    pairs.append((dst[:, 1024:2048].rearrange("p (n i t) -> p n t i", i=4, t=4), src[:, :, 256:512].rearrange("p t (n i) -> p n t i", i=4)))
+            if c < 4 and engine == "vector":
+                pairs.append((dst.rearrange("p (f h c t) -> p f h c t", f=2, h=4, t=4), src.rearrange("p t (h f c) -> p f h c t", f=2, c=64)))
+            elif c < 4:
+                sv = src.rearrange("p t (h f c) -> p f h c t", f=2, c=64)
+                for f in range(2):
+                    pairs.append((dst[:, 1024 * f : 1024 * (f + 1)].rearrange("p (h c t) -> p h c t", h=4, t=4), sv[:, f]))
+            else:
+                sv = src[:, :, 0:256].rearrange("p t (h f c) -> p f h c t", f=2, c=64)
+                for f in range(2):
+                    pairs.append((dst[:, 512 * f : 512 * (f + 1)].rearrange("p (h c t) -> p h c t", h=2, t=4), sv[:, f]))
+                pairs.append((dst[:, 1024:2048].rearrange("p (n t) -> p n t", t=4), src[:, :, 256:512].rearrange("p t n -> p n t")))
             for n, (d, s) in enumerate(pairs):
                 if n not in parts:
                     continue
@@ -182,7 +174,7 @@ def tile_selfattention_pa_kernel(
 
         keep_warm(5)
         for gt in range(8):
-            widen(0, gt, gt in (0, 1, 4))
+            widen(0, gt, gt in (0, 1))
         turn_cache()
         keep_warm(6)
 
@@ -237,7 +229,7 @@ def tile_selfattention_pa_kernel(
         interleave(0, 1, own[:, 1, :], "vector")
         quantize_w(0, 1)
         ctp0 = table_half(0)
-        for gt in range(1, 1 + 1):
+        for gt in range(0, 0 + 1):
             widen(1, gt, False)
         table_copy(ctp0, 0)
         keep_warm(0)
@@ -250,9 +242,9 @@ def tile_selfattention_pa_kernel(
         for i in range(4, 6):
             xts.append(hidden_tile(i))
         keep_warm(0)
-        for gt in range(1):
+        for gt in range(0):
             widen(1, gt, True)
-        for gt in range(1 + 1, 4):
+        for gt in range(0 + 1, 4):
             widen(1, gt, False)
         stage_buf = stream.tile([P, 2048], BF16, name="turn", tag="turn", align_bytes=64, bufs=1)
         interleave(1, 0, stage_buf[:], "gpsimd")

@@ -103,6 +103,38 @@ def tile_selfattention_pa_kernel(
             else:
                 nc.scalar.activation(out=dst, in_=src, func=ACT.Copy, scale=wsc[:, gt : gt + 1])
 
+        half_of = {}
+
+        def interleave_half(c, g, half, engine):
+            hb = stream.tile([P, 1024], BF16, name="half%d" % half, tag="half%d" % half, align_bytes=64, bufs=1)
+            half_of[(c, g, half)] = hb
+            src = planes_of[c][:, 4 * g : 4 * g + 4, :]
+            todo = []
+            if c < 4:
+                sv = src.rearrange("p t (h f c) -> p f h c t", f=2, c=64)
+                todo.append((hb[:].rearrange("p (h c t) -> p h c t", h=4, t=4), sv[:, half]))
+            elif half == 0:
+                sv = src[:, :, 0:256].rearrange("p t (h f c) -> p f h c t", f=2, c=64)
+                for f in range(2):
+                    todo.append((hb[:, 512 * f : 512 * (f + 1)].rearrange("p (h c t) -> p h c t", h=2, t=4), sv[:, f]))
+            else:
+                todo.append((hb[:].rearrange("p (n t) -> p n t", t=4), src[:, :, 256:512].rearrange("p t n -> p n t")))
+            for d, s in todo:
+                if engine == "scalar":
+                    nc.scalar.copy(out=d, in_=s)
+                else:
+                    nc.gpsimd.tensor_scalar(out=d, in0=s, scalar1=1.0, scalar2=0.0, op0=ALU.mult, op1=ALU.add)
+
+        def quantize_half(c, g, half):
+            if c not in codes_of:
+                wc = stream.tile([P, 2, 512], U32, name="wcodes", tag="wcodes", align_bytes=64, bufs=5)
+                wsl = stream.tile([P, 2, 512], U8, name="wscales", tag="wscales", align_bytes=64, bufs=5)
+                codes_of[c] = (wc, wsl)
+            cols = slice(256 * half, 256 * (half + 1))
+            nc.vector.quantize_mx(
+                out=codes_of[c][0][:, g, cols].bitcast(FP8X4), scales=codes_of[c][1][:, g, cols], in_=half_of[(c, g, half)][:]
+            )
+
         def interleave(c, g, dst, engine, parts=(0, 1, 2)):
             grouped_of[(c, g)] = dst
             src = planes_of[c][:, 4 * g : 4 * g + 4, :]
@@ -246,11 +278,12 @@ def tile_selfattention_pa_kernel(
             widen(1, gt, True)
         for gt in range(0 + 1, 4):
             widen(1, gt, False)
-        stage_buf = stream.tile([P, 2048], BF16, name="turn", tag="turn", align_bytes=64, bufs=1)
-        interleave(1, 0, stage_buf[:], "gpsimd")
+        for half in range(2):
+            interleave_half(1, 0, half, "gpsimd")
         for i in range(4, 6):
             hidden_copy(xts[i], i)
-        widen(1, 4, False)
+        for gt in range(4, 4 + 2):
+            widen(1, gt, False)
 
         q_view = out_0.rearrange("o h (p i) c -> p (o h) (i c)", i=8)
         k_view = out_1.rearrange("o h (p i) c -> p (o h) (i c)", i=8)
@@ -348,8 +381,11 @@ def tile_selfattention_pa_kernel(
                         pq = prev["q"]
                         nc.sync.dma_start(out=q_view[:, 4 * pc + 2 * j : 4 * pc + 2 * j + 2, 512 * pq : 512 * (pq + 1)], in_=flat[:, 2 * j : 2 * j + 2])
                     else:
-                        rot_evac(ybs[j], pres[:, :, 4 * j : 4 * j + 4, 0:64])
-                        nc.sync.dma_start(out=k_view[:, :, 512 * j : 512 * (j + 1)], in_=flat[:, :, 512 * j : 512 * (j + 1)])
+                        for e in range(2):
+                            w = 4 // 2
+                            i0 = 4 * j + w * e
+                            nc.scalar.copy(out=pres[:, :, i0 : i0 + w, 0:64].rearrange("p h i c -> p i h c"), in_=ybs[j][:, w * e : w * e + w].rearrange("p i (h c) -> p i h c", c=64))
+                            nc.sync.dma_start(out=k_view[:, :, 128 * i0 : 128 * (i0 + w)], in_=flat[:, :, 128 * i0 : 128 * (i0 + w)])
 
         prev = None
         for k in range(len(slots)):
@@ -389,42 +425,42 @@ def tile_selfattention_pa_kernel(
                 for i in range(6, 8):
                     hidden_copy(xts[i], i)
                 table_copy(ctp1, 1)
-                for gt in range(5, 8 - 1):
+                for gt in range(4 + 2, 8 - 1):
                     widen(1, gt, False)
                 for gt in range(4):
                     widen(2, gt, False)
-            sl["abs"] = [rot_mul(banks[j], *sl["ropes"][j]) for j in range(len(banks))]
-            if k == 0:
-                for bank, out_ap, bias_ap in adds:
-                    pass_add(bank, out_ap, bias_ap)
-                adds = []
-                if 1:
-                    for gt in range(8 - 1, 8):
-                        widen(1, gt, True)
-                quantize_w(order[1], 0)
-                quantize_h(1, 0)
-                quantize_h(1, 1)
-                if not 1:
-                    for gt in range(8 - 1, 8):
-                        widen(1, gt, True)
-            if 0 < k < 8:
-                quantize_w(order[1 + k // 2], k % 2)
-            if k < 7:
-                stage_buf = stream.tile([P, 2048], BF16, name="turn", tag="turn", align_bytes=64, bufs=1)
-                n_s = (0,0,0,0,0,0,3,3)[k + 1]
-                cn = order[1 + (k + 1) // 2]
-                n_parts = 2 if cn < 4 else 3
-                interleave(cn, (k + 1) % 2, stage_buf[:], "gpsimd", range(0, n_parts - n_s))
+            sl["abs"] = []
             n_add = 0
-            for bank, out_ap, bias_ap in adds:
-                pass_add(bank, out_ap, bias_ap)
-                if sl["kind"] == "v":
-                    nc.sync.dma_start(
-                        out=v_view[:, :, 256 * n_add : 256 * (n_add + 1)],
-                        in_=res[:].rearrange("p h i c -> p h (i c)")[:, :, 256 * n_add : 256 * (n_add + 1)],
-                    )
-                n_add += 1
-            if k < 7:
-                interleave(cn, (k + 1) % 2, stage_buf[:], "scalar", range(n_parts - n_s, n_parts))
+            stage = (order[1 + k // 2], k % 2) if k < 8 else None
+            nxt = (order[1 + (k + 1) // 2], (k + 1) % 2) if k < 7 else None
+            on_s = k + 1 >= 9
+            seq = "abddwABh" if k == 0 else "abABdd" if k < 8 else "abdd" if sl["kind"] == "k" else "dddd"
+            for tok in seq:
+                if tok in "ab":
+                    j = "ab".index(tok)
+                    sl["abs"].append(rot_mul(banks[j], *sl["ropes"][j]))
+                elif tok in "AB":
+                    half = "AB".index(tok)
+                    quantize_half(*stage, half)
+                    if nxt is not None and not on_s:
+                        interleave_half(*nxt, half, "gpsimd")
+                elif tok == "w":
+                    for gt in range(8 - 1, 8):
+                        widen(1, gt, True)
+                elif tok == "h":
+                    quantize_h(1, 0)
+                    quantize_h(1, 1)
+                else:
+                    bank, out_ap, bias_ap = adds[n_add]
+                    pass_add(bank, out_ap, bias_ap)
+                    if sl["kind"] == "v":
+                        nc.sync.dma_start(
+                            out=v_view[:, :, 256 * n_add : 256 * (n_add + 1)],
+                            in_=res[:].rearrange("p h i c -> p h (i c)")[:, :, 256 * n_add : 256 * (n_add + 1)],
+                        )
+                    n_add += 1
+            if nxt is not None and on_s:
+                for half in range(2):
+                    interleave_half(*nxt, half, "scalar")
             prev = sl
         turn_back(prev)

@@ -77,10 +77,13 @@ def tile_selfattention_pa_kernel(
         load_x(2)
         load_w(1, 0)
         load_x(3)
-        load_w(1, 1)
         bias_bc = const.tile([P, 2560], BF16, name="bias_bc")
-        nc.sync.dma_start(out=bias_bc[:], in_=b_qkv.partition_broadcast(P))
-        for c in (0, 1, 2, 3, 4)[2:]:
+        nc.sync.dma_start(out=bias_bc[:, 0:512], in_=b_qkv[0:512].partition_broadcast(P))
+        load_w(1, 1)
+        for g in range(2):
+            load_w(2, g)
+        nc.sync.dma_start(out=bias_bc[:, 512:2560], in_=b_qkv[512:2560].partition_broadcast(P))
+        for c in (3, 4):
             for g in range(2):
                 load_w(c, g)
 

from contextlib import ExitStack

import concourse.mybir as mybir
from concourse.masks import make_identity

F32 = mybir.dt.float32
BF16 = mybir.dt.bfloat16
U32 = mybir.dt.uint32
I32 = mybir.dt.int32
U8 = mybir.dt.uint8
FP8 = mybir.dt.float8_e4m3fn
FP8X4 = mybir.dt.float8_e4m3fn_x4
ALU = mybir.AluOpType
ACT = mybir.ActivationFunctionType

P = 128
FLOPS = 2 * 1024 * 1024 * 2560


def tile_selfattention_pa_kernel(
    tc, hidden_states, rope_cache, w_qkv_bytes, w_qkv_scale, b_qkv, out_0, out_1, out_2
):
    nc = tc.nc
    with ExitStack() as ctx:
        const = ctx.enter_context(tc.tile_pool(name="const", bufs=1))
        stream = ctx.enter_context(tc.tile_pool(name="stream", bufs=2))
        psum = ctx.enter_context(tc.psum_pool(name="psum", bufs=2))
        ctx.enter_context(tc.manual_schedule())

        zero = const.tile([P, 512], BF16, name="zero")
        nc.vector.memset(zero[:].bitcast(I32), 0)
        bsel = const.tile([P, P], BF16, name="bsel")
        nc.vector.memset(bsel[:].bitcast(I32), 0)
        warm = const.tile([P, 2], F32, name="warm")
        nc.vector.memset(warm[:, 0:1], 0.0)
        nc.scalar.activation(out=warm[:, 1:2], in_=warm[:, 0:1], func=ACT.Copy)

        cs = const.tile([P, 8, 64], BF16, name="cs")
        nc.sync.dma_start(out=cs[:], in_=rope_cache.rearrange("o (p i) j e -> (o p) i (j e)", i=8))
        wsc = const.tile([P, 8], F32, name="wsc")
        nc.sync.dma_start(
            out=wsc[:].rearrange("p (g t) -> p g t", g=2),
            in_=w_qkv_scale.rearrange("(g p t) o -> p g (t o)", p=P, t=4),
        )

        w_view = w_qkv_bytes.rearrange("(g p t) n -> g p t n", p=P, t=4)
        wb = {}

        for c in range(5):
            wt = const.tile([P, 8, 512], U8, name="wbytes%d" % c)
            wb[c] = wt

        def load_w(c, g):
            cols = slice(512 * c, 512 * (c + 1))
            if c == 0 and g == 0:
                for e in range(2):
                    nc.sync.dma_start(out=wb[c][:, e:4:2, :], in_=w_view[g, :, e:4:2, cols])
            else:
                nc.sync.dma_start(out=wb[c][:, 4 * g : 4 * g + 4, :], in_=w_view[g, :, :, cols])

        x_view = hidden_states.rearrange("o (p i) k -> (o p) i k", i=8)
        xs = []

        def load_x(h):
            t = const.tile([P, 2, 1024], BF16, name="xs%d" % h)
            nc.sync.dma_start(out=t[:], in_=x_view[:, 2 * h : 2 * h + 2, :])
            xs.append(t)

        load_w(0, 0)
        load_w(0, 1)
        load_x(0)
        load_x(1)
        nc.sync.dma_start(
            out=bsel[0:9, :].rearrange("r (hh c) -> r hh c", hh=2),
            in_=b_qkv[0:2304].rearrange("(r hh f c) -> r hh f c", hh=2, f=2, c=64)[:, :, 0, :],
        )
        load_x(2)
        load_w(1, 0)
        load_x(3)
        bias_bc = const.tile([P, 2560], BF16, name="bias_bc")
        nc.sync.dma_start(out=bias_bc[:, 0:512], in_=b_qkv[0:512].partition_broadcast(P))
        load_w(1, 1)
        for g in range(2):
            load_w(2, g)
        nc.sync.dma_start(out=bias_bc[:, 512:2560], in_=b_qkv[512:2560].partition_broadcast(P))
        for c in (3, 4):
            for g in range(2):
                load_w(c, g)

        ident_b = const.tile([P, P], BF16, name="ident_b")
        make_identity(nc, ident_b[:])
        ident_f = const.tile([P, P], F32, name="ident_f")
        make_identity(nc, ident_f[:])

        planes_of = {}
        grouped_of = {}
        codes_of = {}

        def widen(c, gt, on_vector):
            if c not in planes_of:
                planes_of[c] = stream.tile([P, 8, 512], BF16, name="planes", tag="planes")
            src = wb[c][:, gt, :].bitcast(FP8)
            dst = planes_of[c][:, gt, :]
            if on_vector:
                nc.vector.tensor_scalar(out=dst, in0=src, scalar1=wsc[:, gt : gt + 1], scalar2=None, op0=ALU.mult)
            else:
                nc.scalar.activation(out=dst, in_=src, func=ACT.Copy, scale=wsc[:, gt : gt + 1])

        half_of = {}

        def interleave_half(c, g, half, engine):
            hb = stream.tile([P, 1024], BF16, name="half%d" % half, tag="half%d" % half, align_bytes=64, bufs=1)
            half_of[(c, g, half)] = hb
            src = planes_of[c][:, 4 * g : 4 * g + 4, :]
            todo = []
            if c < 4:
                sv = src.rearrange("p t (h f c) -> p f h c t", f=2, c=64)
                todo.append((hb[:].rearrange("p (h c t) -> p h c t", h=4, t=4), sv[:, half]))
            elif half == 0:
                sv = src[:, :, 0:256].rearrange("p t (h f c) -> p f h c t", f=2, c=64)
                for f in range(2):
                    todo.append((hb[:, 512 * f : 512 * (f + 1)].rearrange("p (h c t) -> p h c t", h=2, t=4), sv[:, f]))
            else:
                todo.append((hb[:].rearrange("p (n t) -> p n t", t=4), src[:, :, 256:512].rearrange("p t n -> p n t")))
            for d, s in todo:
                if engine == "scalar":
                    nc.scalar.copy(out=d, in_=s)
                else:
                    nc.gpsimd.tensor_scalar(out=d, in0=s, scalar1=1.0, scalar2=0.0, op0=ALU.mult, op1=ALU.add)

        def quantize_half(c, g, half):
            if c not in codes_of:
                wc = stream.tile([P, 2, 512], U32, name="wcodes", tag="wcodes", align_bytes=64, bufs=5)
                wsl = stream.tile([P, 2, 512], U8, name="wscales", tag="wscales", align_bytes=64, bufs=5)
                codes_of[c] = (wc, wsl)
            cols = slice(256 * half, 256 * (half + 1))
            nc.vector.quantize_mx(
                out=codes_of[c][0][:, g, cols].bitcast(FP8X4), scales=codes_of[c][1][:, g, cols], in_=half_of[(c, g, half)][:]
            )

        def interleave(c, g, dst, engine, parts=(0, 1, 2)):
            grouped_of[(c, g)] = dst
            src = planes_of[c][:, 4 * g : 4 * g + 4, :]
            pairs = []
            if c < 4 and engine == "vector":
                pairs.append((dst.rearrange("p (f h c t) -> p f h c t", f=2, h=4, t=4), src.rearrange("p t (h f c) -> p f h c t", f=2, c=64)))
            elif c < 4:
                sv = src.rearrange("p t (h f c) -> p f h c t", f=2, c=64)
                for f in range(2):
                    pairs.append((dst[:, 1024 * f : 1024 * (f + 1)].rearrange("p (h c t) -> p h c t", h=4, t=4), sv[:, f]))
            else:
                sv = src[:, :, 0:256].rearrange("p t (h f c) -> p f h c t", f=2, c=64)
                for f in range(2):
                    pairs.append((dst[:, 512 * f : 512 * (f + 1)].rearrange("p (h c t) -> p h c t", h=2, t=4), sv[:, f]))
                pairs.append((dst[:, 1024:2048].rearrange("p (n t) -> p n t", t=4), src[:, :, 256:512].rearrange("p t n -> p n t")))
            for n, (d, s) in enumerate(pairs):
                if n not in parts:
                    continue
                if engine == "vector":
                    nc.vector.tensor_copy(out=d, in_=s)
                elif engine == "scalar":
                    nc.scalar.copy(out=d, in_=s)
                else:
                    nc.gpsimd.tensor_scalar(out=d, in0=s, scalar1=1.0, scalar2=0.0, op0=ALU.mult, op1=ALU.add)

        def quantize_w(c, g):
            if c not in codes_of:
                wc = stream.tile([P, 2, 512], U32, name="wcodes", tag="wcodes", align_bytes=64, bufs=5)
                wsl = stream.tile([P, 2, 512], U8, name="wscales", tag="wscales", align_bytes=64, bufs=5)
                codes_of[c] = (wc, wsl)
            nc.vector.quantize_mx(
                out=codes_of[c][0][:, g, :].bitcast(FP8X4), scales=codes_of[c][1][:, g, :], in_=grouped_of[(c, g)]
            )

        own = const.tile([P, 2, 2048], BF16, name="own", align_bytes=64)

        pick = const.tile([P, 2, 2, P], BF16, name="pick")
        id4 = ident_b[:].rearrange("p (i2 j e) -> p i2 j e", i2=2, e=2)
        for s in range(2):
            nc.gpsimd.tensor_scalar(
                out=pick[:, 0, s, :].rearrange("p (hh j e) -> p hh j e", hh=2, e=2),
                in0=id4[:, s, :, 0].unsqueeze(1).unsqueeze(3).to_broadcast([P, 2, 32, 2]),
                scalar1=1.0, scalar2=0.0, op0=ALU.mult, op1=ALU.add,
            )
            for e in range(2):
                nc.gpsimd.tensor_scalar(
                    out=pick[:, 1, s, :].rearrange("p (hh j e) -> p e hh j", hh=2, e=2)[:, e],
                    in0=id4[:, s, :, 1].unsqueeze(1).to_broadcast([P, 2, 32]),
                    scalar1=(1.0 if e == 0 else -1.0), scalar2=0.0, op0=ALU.mult, op1=ALU.add,
                )
        perm_f = const.tile([P, P], F32, name="perm_f")
        id_pairs = ident_f[:].rearrange("p (m e) -> p m e", e=2)
        pm_pairs = perm_f[:].rearrange("p (m e) -> p m e", e=2)
        nc.gpsimd.tensor_copy(out=pm_pairs[:, :, 0], in_=id_pairs[:, :, 1])
        nc.gpsimd.tensor_copy(out=pm_pairs[:, :, 1], in_=id_pairs[:, :, 0])

        csT = const.tile([P, 4, P], BF16, name="csT")

        def keep_warm(n, tag="rot", bufs=2):
            for _ in range(n):
                wt = psum.tile([P, 512], F32, name="wt", tag=tag, bufs=bufs)
                nc.tensor.matmul(out=wt[:], lhsT=zero[:, 0:P], rhs=zero[:], start=True, stop=True)

        def turn_cache():
            cp = psum.tile([P, 4, P], BF16, name="cp", tag="pass")
            for s2 in range(4):
                nc.tensor.transpose(cp[:, s2, :], cs[:, 2 * s2 : 2 * s2 + 2, :].rearrange("p i c -> p (i c)"), ident_b[:])
            nc.vector.tensor_copy(out=csT[:], in_=cp[:])

        keep_warm(5)
        for gt in range(8):
            widen(0, gt, gt in (0, 1))
        turn_cache()
        keep_warm(6)

        h_codes = const.tile([P, 2, 1024], U32, name="h_codes", align_bytes=64)
        h_scales = const.tile([P, 2, 1024], U8, name="h_scales", align_bytes=64)
        ct = const.tile([P, 2, 2, 512], BF16, name="ct")
        hgs = []
        for q in range(2):
            hg = const.tile([P, 2, 4, P, 2], F32, name="hg%d" % q, align_bytes=64)
            hgs.append(hg)

        def hidden_tile(i):
            words = xs[i // 2][:, i % 2, :].bitcast(F32)
            xt = psum.tile([P, 2, 2, P], F32, name="xt", tag="back", bufs=4)
            for g in range(2):
                for u in range(2):
                    nc.tensor.transpose(xt[:, g, u, :], words[:, 256 * g + u : 256 * (g + 1) : 2], ident_f[:])
            return xt

        def hidden_copy(xt, i):
            nc.scalar.copy(out=hgs[i // 4][:, :, i % 4, :, :], in_=xt[:].rearrange("p g u r -> p g r u"))

        def quantize_h(q, g):
            nc.vector.quantize_mx(
                out=h_codes[:, g, 512 * q : 512 * (q + 1)].bitcast(FP8X4),
                scales=h_scales[:, g, 512 * q : 512 * (q + 1)],
                in_=hgs[q][:, g].rearrange("p i r u -> p (i r u)").bitcast(BF16),
            )

        def table_half(q):
            ctp = psum.tile([P, 2, 4, P], BF16, name="ctp", tag=("pass" if q == 0 else "rot"))
            for tb in range(2):
                for i4 in range(4):
                    nc.tensor.matmul(out=ctp[:, tb, i4, :], lhsT=pick[:, tb, i4 % 2, :], rhs=csT[:, 2 * q + i4 // 2, :], start=True, stop=True)
            return ctp

        def table_copy(ctp, q):
            nc.scalar.copy(out=ct[:, q], in_=ctp[:].rearrange("p b i r -> p b (i r)"))

        xts = []
        for i in range(2):
            xts.append(hidden_tile(i))
        keep_warm(2)
        for i in range(2, 4):
            xts.append(hidden_tile(i))
        keep_warm(2)
        for i in range(4):
            hidden_copy(xts[i], i)

        interleave(0, 0, own[:, 0, :], "vector")
        quantize_w(0, 0)
        interleave(0, 1, own[:, 1, :], "vector")
        quantize_w(0, 1)
        ctp0 = table_half(0)
        for gt in range(0, 0 + 1):
            widen(1, gt, False)
        table_copy(ctp0, 0)
        keep_warm(0)
        quantize_h(0, 0)
        quantize_h(0, 1)
        b_rot = const.tile([P, 9], BF16, name="b_rot")
        btp = psum.tile([P, P], BF16, name="btp", tag="rot")
        nc.tensor.transpose(btp[:], bsel[:], ident_b[:])
        nc.vector.tensor_copy(out=b_rot[:], in_=btp[:, 0:9])
        for i in range(4, 6):
            xts.append(hidden_tile(i))
        keep_warm(0)
        for gt in range(0):
            widen(1, gt, True)
        for gt in range(0 + 1, 4):
            widen(1, gt, False)
        for half in range(2):
            interleave_half(1, 0, half, "gpsimd")
        for i in range(4, 6):
            hidden_copy(xts[i], i)
        for gt in range(4, 4 + 2):
            widen(1, gt, False)

        q_view = out_0.rearrange("o h (p i) c -> p (o h) (i c)", i=8)
        k_view = out_1.rearrange("o h (p i) c -> p (o h) (i c)", i=8)
        v_view = out_2.rearrange("o h (p i) c -> p (o h) (i c)", i=8)

        def mx_group(out, lhsT, lhsT_s, rhs, rhs_s):
            for g in range(2):
                nc.tensor.matmul_mx(
                    out=out,
                    lhsT=lhsT(g).bitcast(FP8X4), lhsT_scale=lhsT_s(g),
                    rhs=rhs(g).bitcast(FP8X4), rhs_scale=rhs_s(g),
                    start=(g == 0), stop=(g == 1),
                )

        def rot_mx(c, rl, q):
            wc, wsl = codes_of[c]
            bank = psum.tile([P, 512], F32, name="rotb", tag="rot")
            mx_group(
                bank[:],
                lambda g: wc[:, g, P * rl : P * (rl + 1)], lambda g: wsl[:, g, P * rl : P * (rl + 1)],
                lambda g: h_codes[:, g, 512 * q : 512 * (q + 1)], lambda g: h_scales[:, g, 512 * q : 512 * (q + 1)],
            )
            return bank

        def rot_mul(bank, c, rl, q):
            r = 2 * c + rl
            ab = stream.tile([P, 2, 512], F32, name="ab", tag="ab", bufs=4)
            nc.vector.scalar_tensor_tensor(
                out=ab[:], in0=bank[:].unsqueeze(1).to_broadcast([P, 2, 512]), scalar=b_rot[:, r : r + 1],
                in1=ct[:, q], op0=ALU.add, op1=ALU.mult,
            )
            return ab

        def rot_back(ab):
            yb = psum.tile([P, 4, P], F32, name="yb", tag="back", bufs=4)
            for i4 in range(4):
                nc.tensor.matmul(out=yb[:, i4, :], lhsT=ab[:, 0, P * i4 : P * (i4 + 1)], rhs=ident_f[:],
                                 is_transpose=True, start=True, stop=False)
                nc.tensor.matmul(out=yb[:, i4, :], lhsT=ab[:, 1, P * i4 : P * (i4 + 1)], rhs=perm_f[:],
                                 is_transpose=True, start=False, stop=True)
            return yb

        def rot_evac(yb, out_ap):
            nc.scalar.copy(out=out_ap.rearrange("p h i c -> p i h c"), in_=yb[:].rearrange("p i (h c) -> p i h c", c=64))

        def pass_mx(c, col0, width, first_i, tag="pass"):
            wc, wsl = codes_of[c]
            n_i = 512 // width
            bank = psum.tile([P, n_i, width], F32, name="passb", tag=tag)
            for ii in range(n_i):
                i = first_i + ii
                mx_group(
                    bank[:, ii, :],
                    lambda g: h_codes[:, g, P * i : P * (i + 1)], lambda g: h_scales[:, g, P * i : P * (i + 1)],
                    lambda g: wc[:, g, col0 : col0 + width], lambda g: wsl[:, g, col0 : col0 + width],
                )
            return bank

        def pass_add(bank, out_ap, bias_ap):
            hc = bias_ap.shape[2]
            n_i = out_ap.shape[2]
            nc.vector.tensor_tensor(
                out=out_ap.rearrange("p h i c -> p i h c"), in0=bank[:].rearrange("p i (h c) -> p i h c", c=hc),
                in1=bias_ap.unsqueeze(1).to_broadcast([P, n_i, bias_ap.shape[1], hc]), op=ALU.add,
            )

        def new_res(shape):
            return stream.tile(shape, F32, name="res", tag="res", bufs=10)

        slots = []
        def add_q(c):
            b_ap = bias_bc[:, 512 * c : 512 * (c + 1)].rearrange("p (h f c) -> p f h c", f=2, c=64)[:, 1]
            for q in range(2):
                slots.append({"c": c, "q": q, "ropes": [(c, 0, q), (c, 1, q)], "kind": "q", "bias": b_ap})

        for c in (0, 1, 2, 3, 4):
            if c < 4:
                add_q(c)
            else:
                slots.append({"c": 4, "kind": "k", "ropes": [(4, 0, 0), (4, 0, 1)]})
                slots.append({"c": 4, "kind": "v", "ropes": []})
        order = (0, 1, 2, 3, 4)
        b_k = bias_bc[:, 2048:2304].rearrange("p (h f c) -> p f h c", f=2, c=64)[:, 1]
        b_v = bias_bc[:, 2304:2560].rearrange("p (h c) -> p h c", c=128)

        def turn_back(prev):
            if prev is not None and prev["ropes"]:
                ybs = [rot_back(ab) for ab in prev["abs"]]
                pres = prev["res"]
                flat = pres[:].rearrange("p h i c -> p h (i c)")
                for j in range(len(ybs)):
                    if prev["kind"] == "q":
                        rot_evac(ybs[j], pres[:, 2 * j : 2 * j + 2, :, 0:64])
                        pc = prev["c"]
                        pq = prev["q"]
                        nc.sync.dma_start(out=q_view[:, 4 * pc + 2 * j : 4 * pc + 2 * j + 2, 512 * pq : 512 * (pq + 1)], in_=flat[:, 2 * j : 2 * j + 2])
                    else:
                        for e in range(2):
                            w = 4 // 2
                            i0 = 4 * j + w * e
                            nc.scalar.copy(out=pres[:, :, i0 : i0 + w, 0:64].rearrange("p h i c -> p i h c"), in_=ybs[j][:, w * e : w * e + w].rearrange("p i (h c) -> p i h c", c=64))
                            nc.sync.dma_start(out=k_view[:, :, 128 * i0 : 128 * (i0 + w)], in_=flat[:, :, 128 * i0 : 128 * (i0 + w)])

        prev = None
        for k in range(len(slots)):
            sl = slots[k]
            c = sl["c"]
            if k >= 8:
                turn_back(prev)
            banks = [rot_mx(*u) for u in sl["ropes"]]
            if 0 < k < 6:
                for t in range(4):
                    widen(order[2 + k // 2], 4 * (k % 2) + t, False)
            if k < 8:
                turn_back(prev)
            adds = []
            if sl["kind"] == "q":
                q = sl["q"]
                res = new_res([P, 4, 4, P])
                sl["res"] = res
                for ipl in range(2):
                    adds.append((pass_mx(c, 256, 256, 4 * q + 2 * ipl), res[:, :, 2 * ipl : 2 * ipl + 2, 64:128], sl["bias"]))
            elif sl["kind"] == "k":
                res = new_res([P, 2, 8, P])
                sl["res"] = res
                for q in range(2):
                    adds.append((pass_mx(4, 128, 128, 4 * q), res[:, :, 4 * q : 4 * q + 4, 64:128], b_k))
            else:
                res = new_res([P, 2, 8, P])
                sl["res"] = res
                for ip in range(4):
                    tag = "pass" if ip < 2 else "rot"
                    adds.append((pass_mx(4, 256, 256, 2 * ip, tag), res[:, :, 2 * ip : 2 * ip + 2, :], b_v))
            if k == 0:
                ctp1 = table_half(1)
                for i in range(6, 8):
                    xts.append(hidden_tile(i))
                keep_warm(3, "back", 4)
                for i in range(6, 8):
                    hidden_copy(xts[i], i)
                table_copy(ctp1, 1)
                for gt in range(4 + 2, 8 - 1):
                    widen(1, gt, False)
                for gt in range(4):
                    widen(2, gt, False)
            sl["abs"] = []
            n_add = 0
            stage = (order[1 + k // 2], k % 2) if k < 8 else None
            nxt = (order[1 + (k + 1) // 2], (k + 1) % 2) if k < 7 else None
            on_s = k + 1 >= 9
            seq = "abddwABh" if k == 0 else "abABdd" if k < 8 else "abdd" if sl["kind"] == "k" else "dddd"
            for tok in seq:
                if tok in "ab":
                    j = "ab".index(tok)
                    sl["abs"].append(rot_mul(banks[j], *sl["ropes"][j]))
                elif tok in "AB":
                    half = "AB".index(tok)
                    quantize_half(*stage, half)
                    if nxt is not None and not on_s:
                        interleave_half(*nxt, half, "gpsimd")
                elif tok == "w":
                    for gt in range(8 - 1, 8):
                        widen(1, gt, True)
                elif tok == "h":
                    quantize_h(1, 0)
                    quantize_h(1, 1)
                else:
                    bank, out_ap, bias_ap = adds[n_add]
                    pass_add(bank, out_ap, bias_ap)
                    if sl["kind"] == "v":
                        nc.sync.dma_start(
                            out=v_view[:, :, 256 * n_add : 256 * (n_add + 1)],
                            in_=res[:].rearrange("p h i c -> p h (i c)")[:, :, 256 * n_add : 256 * (n_add + 1)],
                        )
                    n_add += 1
            if nxt is not None and on_s:
                for half in range(2):
                    interleave_half(*nxt, half, "scalar")
            prev = sl
        turn_back(prev)
